import numpy as np
import ml_dtypes


def mxq(x, axis, fmt="e4m3"):
    dtype, down = {"e4m3": (ml_dtypes.float8_e4m3fn, 7), "e5m2": (ml_dtypes.float8_e5m2, 14)}[fmt]
    v = np.moveaxis(np.asarray(x, np.float32).astype(ml_dtypes.bfloat16).astype(np.float64), axis, -1)
    blocks = v.reshape(v.shape[:-1] + (-1, 32))
    amax = np.abs(blocks).max(-1, keepdims=True)
    byte = np.maximum(np.where(amax > 0, np.frexp(amax)[1] - 1 + 127, 0) - down, 1)
    scale = np.exp2(byte - 127.0)
    codes = (blocks / scale).astype(np.float32).astype(dtype).astype(np.float64)
    return np.moveaxis((codes * scale).reshape(v.shape), -1, axis)


WIDE = False


def mx_kscale(k):
    if not WIDE:
        return np.ones(k)
    levels = np.array([10, -10, 5, -5, 0])
    a = np.random.permutation(np.resize(levels, k // 512 * 4)).reshape(k // 512, 4)
    idx = np.arange(k)
    return np.exp2(a[idx // 512, idx % 128 // 32])


BF16 = ml_dtypes.bfloat16


def bf(x):
    return np.asarray(x, np.float32).astype(BF16)


def f64(x):
    return np.asarray(x).astype(np.float64)


B, L, C, K = 64, 2, 512, 5
F = C
BN_EPS = 1e-3
LEAKY_ALPHA = 0.3


def leaky(v):
    return np.where(v >= 0, v, LEAKY_ALPHA * v)


def bn(v, gamma, beta, mean, var):
    return gamma * (v - mean) * (1.0 / np.sqrt(var + BN_EPS)) + beta


def setup_inputs():
    s = mx_kscale(F)
    return {"h": bf(leaky(np.random.standard_normal((B, L, F)) * 1.2) * s),
            "x": bf(np.random.standard_normal((B, L, C))),
            "k2": bf(np.random.standard_normal((K, L, F, F)) * 0.16 / np.sqrt(K * F) / s[:, None]),
            "b2": bf(np.random.standard_normal((L, F)) * 0.03),
            "gamma2": bf(1.0 + 0.1 * np.random.standard_normal(F)),
            "beta2": bf(np.random.standard_normal(F) * 0.2),
            "mean2": bf(np.random.standard_normal(F) * 0.05),
            "var2": bf(np.random.uniform(0.01, 0.03, F))}


def reference(h, x, k2, b2, gamma2, beta2, mean2, var2):
    hq = mxq(f64(h).transpose(1, 0, 2), 2, "e4m3")
    k = f64(k2)
    out = 2.0 * f64(b2)
    for i in range(k.shape[0]):
        step = (i // 2) * (-1 if i % 2 == 1 else 1)
        ki = np.roll(k[i], -step, axis=0) if step != 0 else k[i]
        p = hq @ mxq(ki, 1, "e4m3")
        p = np.roll(p, step, axis=0) if step != 0 else p
        out = out + p.transpose(1, 0, 2)
    return leaky(bn(out, f64(gamma2), f64(beta2), f64(mean2), f64(var2)) + f64(x))

@@ -1,0 +1,166 @@
+from contextlib import ExitStack
+
+import concourse.mybir as mybir
+from concourse.masks import make_identity
+
+F32 = mybir.dt.float32
+BF16 = mybir.dt.bfloat16
+U32 = mybir.dt.uint32
+U8 = mybir.dt.uint8
+FP8X4 = mybir.dt.float8_e4m3fn_x4
+ALU = mybir.AluOpType
+
+P = 128
+PACK = 4
+B, L, C, TAPS = 64, 2, 512, 5
+ROWS = B * L
+STEPS = (0, 0, 1, -1, 2)
+CHUNKS = C // P
+BN_EPS = 1e-3
+LEAKY_ALPHA = 0.3
+RUN = 4
+SCALAR_COLS = 320
+HALF = C // 2
+
+FLOPS = 2 * B * L * TAPS * C * C
+
+
+def regroup(copy, grouped, raw, cols):
+    copy(
+        out=grouped[:, cols, :].rearrange("p (c i) t -> p c t i", i=RUN),
+        in_=raw[:, :, cols].rearrange("p t (c i) -> p c t i", i=RUN),
+    )
+
+
+def tile_residualblock5_pb_s_kernel(tc, h, x, k2, b2, gamma2, beta2, mean2, var2, out):
+    nc = tc.nc
+    with ExitStack() as ctx:
+        keep = ctx.enter_context(tc.tile_pool(name="keep", bufs=1))
+        stage = ctx.enter_context(tc.tile_pool(name="stage", bufs=3))
+        psum = ctx.enter_context(tc.psum_pool(name="psum", bufs=1))
+
+        h_rows = keep.tile([ROWS, C], BF16)
+        nc.sync.dma_start(out=h_rows[:], in_=h.rearrange("b l c -> (b l) c"))
+
+        params = keep.tile([P, C], BF16)
+        nc.vector.memset(params[:], 0.0)
+        for row, vec in enumerate((gamma2, beta2, mean2, var2)):
+            nc.scalar.dma_start(out=params[row : row + 1, :], in_=vec.unsqueeze(0))
+        nc.scalar.dma_start(out=params[4:6, :], in_=b2)
+        x_rows = keep.tile([ROWS, C], BF16)
+        nc.scalar.dma_start(out=x_rows[:], in_=x.rearrange("b l c -> (b l) c"))
+
+        kernels = [(i, l) for i in range(TAPS) for l in range(L)]
+        w_raw = []
+        for m, (i, l) in enumerate(kernels):
+            raw = keep.tile([P, PACK, C], BF16, name="w_raw%d" % m)
+            nc.sync.dma_start(out=raw[:], in_=k2[i, l].rearrange("(p t) f -> p t f", t=PACK))
+            w_raw.append(raw)
+
+        ident_f32 = keep.tile([P, P], F32)
+        make_identity(nc, ident_f32[:])
+        ident_bf16 = keep.tile([P, P], BF16)
+        make_identity(nc, ident_bf16[:])
+
+        h_words = h_rows[:].bitcast(F32).rearrange("r (p u) -> r u p", u=2)
+        h_grouped = keep.tile([P, L * L * ROWS * PACK], BF16, align_bytes=64)
+        nc.vector.memset(h_grouped[:], 0.0)
+        h_grouped_words = h_grouped[:].bitcast(F32).rearrange(
+            "p (o s b l u) -> p o s b l u", o=L, s=L, b=B, l=L, u=2
+        )
+        copies = (nc.vector.tensor_copy, nc.scalar.copy)
+        for o in range(L):
+            h_T = psum.tile([P, 2, ROWS], F32, name="h_T%d" % o)
+            for u in range(2):
+                nc.tensor.transpose(h_T[:, u, :], h_words[:, u, :], ident_f32[:])
+            copies[o](
+                out=h_grouped_words[:, o, :, :, o, :],
+                in_=h_T[:].rearrange("p u (b s) -> p s b u", s=L),
+            )
+        h_codes = keep.tile([P, L * L * ROWS], U32, align_bytes=64)
+        h_scales = keep.tile([P, L * L * ROWS], U8, align_bytes=64)
+        nc.vector.quantize_mx(out=h_codes[:].bitcast(FP8X4), scales=h_scales[:], in_=h_grouped[:])
+
+        params_T = psum.tile([P, CHUNKS, P], BF16)
+        for m in range(CHUNKS):
+            nc.tensor.transpose(params_T[:, m, :], params[:, m * P : (m + 1) * P], ident_bf16[:])
+        pvals = keep.tile([P, 6, CHUNKS], F32)
+        nc.vector.tensor_copy(out=pvals[:], in_=params_T[:, :, 0:6].rearrange("p m v -> p v m"))
+        gamma_c, beta_c, mean_c, var_c = pvals[:, 0, :], pvals[:, 1, :], pvals[:, 2, :], pvals[:, 3, :]
+        b2_c = pvals[:, 4:6, :].rearrange("p l m -> p m l")
+
+        var_eps = keep.tile([P, CHUNKS], F32)
+        nc.vector.tensor_scalar_add(out=var_eps[:], in0=var_c, scalar1=BN_EPS)
+        std = keep.tile([P, CHUNKS], F32)
+        nc.scalar.sqrt(out=std[:], in_=var_eps[:])
+        rstd = keep.tile([P, CHUNKS], F32)
+        nc.vector.reciprocal(out=rstd[:], in_=std[:])
+        gain = keep.tile([P, CHUNKS], F32)
+        nc.vector.tensor_mul(out=gain[:], in0=gamma_c, in1=rstd[:])
+        centred = keep.tile([P, CHUNKS, L], F32)
+        nc.vector.scalar_tensor_tensor(
+            out=centred[:],
+            in0=b2_c,
+            scalar=2.0,
+            in1=mean_c.unsqueeze(2).to_broadcast([P, CHUNKS, L]),
+            op0=ALU.mult,
+            op1=ALU.subtract,
+        )
+        scaled = keep.tile([P, CHUNKS, L], F32)
+        nc.vector.tensor_mul(out=scaled[:], in0=centred[:], in1=gain[:].unsqueeze(2).to_broadcast([P, CHUNKS, L]))
+        shift = keep.tile([P, CHUNKS, L], F32)
+        nc.vector.tensor_add(out=shift[:], in0=scaled[:], in1=beta_c.unsqueeze(2).to_broadcast([P, CHUNKS, L]))
+
+        gain_rep = keep.tile([P, CHUNKS, ROWS], F32)
+        nc.vector.tensor_copy(out=gain_rep[:], in_=gain[:].unsqueeze(2).to_broadcast([P, CHUNKS, ROWS]))
+        shift_rep = keep.tile([P, CHUNKS, B, L], F32)
+        nc.vector.tensor_copy(out=shift_rep[:], in_=shift[:].unsqueeze(2).to_broadcast([P, CHUNKS, B, L]))
+        gain_ps = psum.tile([ROWS, C], F32)
+        shift_ps = psum.tile([ROWS, C], F32)
+        for m in range(CHUNKS):
+            nc.tensor.transpose(gain_ps[:, m * P : (m + 1) * P], gain_rep[:, m, :], ident_f32[:])
+        for m in range(CHUNKS):
+            nc.tensor.transpose(
+                shift_ps[:, m * P : (m + 1) * P], shift_rep[:, m].rearrange("p b l -> p (b l)"), ident_f32[:]
+            )
+        gain_rows = keep.tile([ROWS, C], F32)
+        nc.scalar.copy(out=gain_rows[:], in_=gain_ps[:])
+        shift_x = keep.tile([ROWS, C], F32)
+        nc.vector.tensor_add(out=shift_x[:], in0=shift_ps[:], in1=x_rows[:])
+
+        y_ps = psum.tile([ROWS, C], F32)
+        for m, (i, l) in enumerate(kernels):
+            grouped = stage.tile([P, C, PACK], BF16, align_bytes=64)
+            regroup(nc.vector.tensor_copy, grouped, w_raw[m], slice(0, C - SCALAR_COLS))
+            regroup(nc.scalar.copy, grouped, w_raw[m], slice(C - SCALAR_COLS, C))
+            w_codes = keep.tile([P, C], U32, name="w_codes%d" % m, align_bytes=64)
+            w_scales = keep.tile([P, C], U8, name="w_scales%d" % m, align_bytes=64)
+            nc.vector.quantize_mx(
+                out=w_codes[:].bitcast(FP8X4),
+                scales=w_scales[:],
+                in_=grouped[:].rearrange("p f t -> p (f t)"),
+            )
+            source = (l - STEPS[i]) % L
+            operand = slice((l * L + source) * ROWS, (l * L + source + 1) * ROWS)
+            nc.tensor.matmul_mx(
+                out=y_ps[:],
+                lhsT=h_codes[:, operand].bitcast(FP8X4),
+                lhsT_scale=h_scales[:, operand],
+                rhs=w_codes[:].bitcast(FP8X4),
+                rhs_scale=w_scales[:],
+                start=(m == 0),
+                stop=(m == len(kernels) - 1),
+            )
+
+        out_rows = out.rearrange("b l f -> (b l) f")
+        for half in range(2):
+            cols = slice(half * HALF, (half + 1) * HALF)
+            gy = stage.tile([ROWS, HALF], F32)
+            nc.vector.tensor_mul(out=gy[:], in0=y_ps[:, cols], in1=gain_rows[:, cols])
+            z = stage.tile([ROWS, HALF], F32)
+            nc.vector.tensor_add(out=z[:], in0=gy[:], in1=shift_x[:, cols])
+            res = stage.tile([ROWS, HALF], F32)
+            nc.vector.scalar_tensor_tensor(
+                out=res[:], in0=z[:], scalar=LEAKY_ALPHA, in1=z[:], op0=ALU.mult, op1=ALU.max
+            )
+            nc.sync.dma_start(out=out_rows[:, cols], in_=res[:])

@@ -19,8 +19,8 @@ CHUNKS = C // P
 BN_EPS = 1e-3
 LEAKY_ALPHA = 0.3
 RUN = 4
-SCALAR_COLS = 320
 HALF = C // 2
+VECTOR_SHARE = (7, 16)
 
 FLOPS = 2 * B * L * TAPS * C * C
 
@@ -36,8 +36,13 @@ def tile_residualblock5_pb_s_kernel(tc, h, x, k2, b2, gamma2, beta2, mean2, var2
     nc = tc.nc
     with ExitStack() as ctx:
         keep = ctx.enter_context(tc.tile_pool(name="keep", bufs=1))
-        stage = ctx.enter_context(tc.tile_pool(name="stage", bufs=3))
+        stage = ctx.enter_context(tc.tile_pool(name="stage", bufs=4))
         psum = ctx.enter_context(tc.psum_pool(name="psum", bufs=1))
+
+        one = keep.tile([P, 1], F32)
+        nc.vector.memset(one[:], 1.0)
+        warm = keep.tile([P, 1], F32)
+        nc.scalar.sqrt(out=warm[:], in_=one[:])
 
         h_rows = keep.tile([ROWS, C], BF16)
         nc.sync.dma_start(out=h_rows[:], in_=h.rearrange("b l c -> (b l) c"))
@@ -128,35 +133,42 @@ def tile_residualblock5_pb_s_kernel(tc, h, x, k2, b2, gamma2, beta2, mean2, var2
         shift_x = keep.tile([ROWS, C], F32)
         nc.vector.tensor_add(out=shift_x[:], in0=shift_ps[:], in1=x_rows[:])
 
-        y_ps = psum.tile([ROWS, C], F32)
-        for m, (i, l) in enumerate(kernels):
+        last = len(kernels) - 1
+        pieces = [(m, 0, C) for m in range(last)] + [(last, 0, HALF), (last, HALF, HALF)]
+        y_ps = [psum.tile([ROWS, HALF], F32, name="y_ps%d" % half) for half in range(2)]
+        w_codes = [keep.tile([P, C], U32, name="w_codes%d" % m, align_bytes=64) for m in range(len(kernels))]
+        w_scales = [keep.tile([P, C], U8, name="w_scales%d" % m, align_bytes=64) for m in range(len(kernels))]
+        for m, first, width in pieces:
+            i, l = kernels[m]
+            vector_cols = width * VECTOR_SHARE[0] // VECTOR_SHARE[1]
             grouped = stage.tile([P, C, PACK], BF16, align_bytes=64)
-            regroup(nc.vector.tensor_copy, grouped, w_raw[m], slice(0, C - SCALAR_COLS))
-            regroup(nc.scalar.copy, grouped, w_raw[m], slice(C - SCALAR_COLS, C))
-            w_codes = keep.tile([P, C], U32, name="w_codes%d" % m, align_bytes=64)
-            w_scales = keep.tile([P, C], U8, name="w_scales%d" % m, align_bytes=64)
+            regroup(nc.vector.tensor_copy, grouped, w_raw[m], slice(first, first + vector_cols))
+            regroup(nc.scalar.copy, grouped, w_raw[m], slice(first + vector_cols, first + width))
+            cols = slice(first, first + width)
             nc.vector.quantize_mx(
-                out=w_codes[:].bitcast(FP8X4),
-                scales=w_scales[:],
-                in_=grouped[:].rearrange("p f t -> p (f t)"),
+                out=w_codes[m][:, cols].bitcast(FP8X4),
+                scales=w_scales[m][:, cols],
+                in_=grouped[:, cols, :].rearrange("p f t -> p (f t)"),
             )
             source = (l - STEPS[i]) % L
             operand = slice((l * L + source) * ROWS, (l * L + source + 1) * ROWS)
-            nc.tensor.matmul_mx(
-                out=y_ps[:],
-                lhsT=h_codes[:, operand].bitcast(FP8X4),
-                lhsT_scale=h_scales[:, operand],
-                rhs=w_codes[:].bitcast(FP8X4),
-                rhs_scale=w_scales[:],
-                start=(m == 0),
-                stop=(m == len(kernels) - 1),
-            )
+            for half in range(first // HALF, (first + width) // HALF):
+                half_cols = slice(half * HALF, (half + 1) * HALF)
+                nc.tensor.matmul_mx(
+                    out=y_ps[half][:],
+                    lhsT=h_codes[:, operand].bitcast(FP8X4),
+                    lhsT_scale=h_scales[:, operand],
+                    rhs=w_codes[m][:, half_cols].bitcast(FP8X4),
+                    rhs_scale=w_scales[m][:, half_cols],
+                    start=(m == 0),
+                    stop=(m == last),
+                )
 
         out_rows = out.rearrange("b l f -> (b l) f")
         for half in range(2):
             cols = slice(half * HALF, (half + 1) * HALF)
             gy = stage.tile([ROWS, HALF], F32)
-            nc.vector.tensor_mul(out=gy[:], in0=y_ps[:, cols], in1=gain_rows[:, cols])
+            nc.vector.tensor_mul(out=gy[:], in0=y_ps[half][:], in1=gain_rows[:, cols])
             z = stage.tile([ROWS, HALF], F32)
             nc.vector.tensor_add(out=z[:], in0=gy[:], in1=shift_x[:, cols])
             res = stage.tile([ROWS, HALF], F32)

@@ -19,8 +19,8 @@ CHUNKS = C // P
 BN_EPS = 1e-3
 LEAKY_ALPHA = 0.3
 RUN = 4
-HALF = C // 2
 VECTOR_SHARE = (7, 16)
+GROUPS = ((0, C // 2), (C // 2, C // 4), (3 * C // 4, C // 4))
 
 FLOPS = 2 * B * L * TAPS * C * C
 
@@ -73,35 +73,71 @@ def tile_residualblock5_pb_s_kernel(tc, h, x, k2, b2, gamma2, beta2, mean2, var2
         h_grouped_words = h_grouped[:].bitcast(F32).rearrange(
             "p (o s b l u) -> p o s b l u", o=L, s=L, b=B, l=L, u=2
         )
-        copies = (nc.vector.tensor_copy, nc.scalar.copy)
+        h_T = psum.tile([P, 2, ROWS], F32)
+        for u in range(2):
+            nc.tensor.transpose(h_T[:, u, :], h_words[:, u, :], ident_f32[:])
         for o in range(L):
-            h_T = psum.tile([P, 2, ROWS], F32, name="h_T%d" % o)
-            for u in range(2):
-                nc.tensor.transpose(h_T[:, u, :], h_words[:, u, :], ident_f32[:])
-            copies[o](
+            nc.scalar.copy(
                 out=h_grouped_words[:, o, :, :, o, :],
                 in_=h_T[:].rearrange("p u (b s) -> p s b u", s=L),
             )
         h_codes = keep.tile([P, L * L * ROWS], U32, align_bytes=64)
         h_scales = keep.tile([P, L * L * ROWS], U8, align_bytes=64)
-        nc.vector.quantize_mx(out=h_codes[:].bitcast(FP8X4), scales=h_scales[:], in_=h_grouped[:])
 
         params_T = psum.tile([P, CHUNKS, P], BF16)
         for m in range(CHUNKS):
             nc.tensor.transpose(params_T[:, m, :], params[:, m * P : (m + 1) * P], ident_bf16[:])
+        x_T = psum.tile([P, CHUNKS, ROWS], BF16)
+        for m in range(CHUNKS):
+            nc.tensor.transpose(x_T[:, m, :], x_rows[:, m * P : (m + 1) * P], ident_bf16[:])
         pvals = keep.tile([P, 6, CHUNKS], F32)
         nc.vector.tensor_copy(out=pvals[:], in_=params_T[:, :, 0:6].rearrange("p m v -> p v m"))
         gamma_c, beta_c, mean_c, var_c = pvals[:, 0, :], pvals[:, 1, :], pvals[:, 2, :], pvals[:, 3, :]
         b2_c = pvals[:, 4:6, :].rearrange("p l m -> p m l")
 
+        last = len(kernels) - 1
+        pieces = [(m, 0, C) for m in range(last)] + [(last, first, width) for first, width in GROUPS]
+        y_ps = [psum.tile([ROWS, width], F32, name="y_ps%d" % g) for g, (first, width) in enumerate(GROUPS)]
+        w_codes = [keep.tile([P, C], U32, name="w_codes%d" % m, align_bytes=64) for m in range(len(kernels))]
+        w_scales = [keep.tile([P, C], U8, name="w_scales%d" % m, align_bytes=64) for m in range(len(kernels))]
+        grouped_of = {}
+
+        def regroup_piece(j):
+            m, first, width = pieces[j]
+            vector_cols = width * VECTOR_SHARE[0] // VECTOR_SHARE[1]
+            grouped = stage.tile([P, C, PACK], BF16, align_bytes=64)
+            regroup(nc.vector.tensor_copy, grouped, w_raw[m], slice(first, first + vector_cols))
+            regroup(nc.scalar.copy, grouped, w_raw[m], slice(first + vector_cols, first + width))
+            grouped_of[j] = grouped
+
+        def quantise_and_multiply_piece(j):
+            m, first, width = pieces[j]
+            i, l = kernels[m]
+            cols = slice(first, first + width)
+            nc.vector.quantize_mx(
+                out=w_codes[m][:, cols].bitcast(FP8X4),
+                scales=w_scales[m][:, cols],
+                in_=grouped_of[j][:, cols, :].rearrange("p f t -> p (f t)"),
+            )
+            source = (l - STEPS[i]) % L
+            operand = slice((l * L + source) * ROWS, (l * L + source + 1) * ROWS)
+            for g, (group_first, group_width) in enumerate(GROUPS):
+                if first <= group_first < first + width:
+                    group_cols = slice(group_first, group_first + group_width)
+                    nc.tensor.matmul_mx(
+                        out=y_ps[g][:],
+                        lhsT=h_codes[:, operand].bitcast(FP8X4),
+                        lhsT_scale=h_scales[:, operand],
+                        rhs=w_codes[m][:, group_cols].bitcast(FP8X4),
+                        rhs_scale=w_scales[m][:, group_cols],
+                        start=(m == 0),
+                        stop=(m == last),
+                    )
+
         var_eps = keep.tile([P, CHUNKS], F32)
         nc.vector.tensor_scalar_add(out=var_eps[:], in0=var_c, scalar1=BN_EPS)
         std = keep.tile([P, CHUNKS], F32)
         nc.scalar.sqrt(out=std[:], in_=var_eps[:])
-        rstd = keep.tile([P, CHUNKS], F32)
-        nc.vector.reciprocal(out=rstd[:], in_=std[:])
-        gain = keep.tile([P, CHUNKS], F32)
-        nc.vector.tensor_mul(out=gain[:], in0=gamma_c, in1=rstd[:])
         centred = keep.tile([P, CHUNKS, L], F32)
         nc.vector.scalar_tensor_tensor(
             out=centred[:],
@@ -111,67 +147,59 @@ def tile_residualblock5_pb_s_kernel(tc, h, x, k2, b2, gamma2, beta2, mean2, var2
             op0=ALU.mult,
             op1=ALU.subtract,
         )
+
+        regroup_piece(0)
+
+        rstd = keep.tile([P, CHUNKS], F32)
+        nc.vector.reciprocal(out=rstd[:], in_=std[:])
+        gain = keep.tile([P, CHUNKS], F32)
+        nc.vector.tensor_mul(out=gain[:], in0=gamma_c, in1=rstd[:])
         scaled = keep.tile([P, CHUNKS, L], F32)
         nc.vector.tensor_mul(out=scaled[:], in0=centred[:], in1=gain[:].unsqueeze(2).to_broadcast([P, CHUNKS, L]))
         shift = keep.tile([P, CHUNKS, L], F32)
         nc.vector.tensor_add(out=shift[:], in0=scaled[:], in1=beta_c.unsqueeze(2).to_broadcast([P, CHUNKS, L]))
 
-        gain_rep = keep.tile([P, CHUNKS, ROWS], F32)
-        nc.vector.tensor_copy(out=gain_rep[:], in_=gain[:].unsqueeze(2).to_broadcast([P, CHUNKS, ROWS]))
-        shift_rep = keep.tile([P, CHUNKS, B, L], F32)
-        nc.vector.tensor_copy(out=shift_rep[:], in_=shift[:].unsqueeze(2).to_broadcast([P, CHUNKS, B, L]))
+        nc.vector.quantize_mx(out=h_codes[:].bitcast(FP8X4), scales=h_scales[:], in_=h_grouped[:])
+
+        shift_x_T = keep.tile([P, CHUNKS, B, L], F32)
+        nc.vector.tensor_add(
+            out=shift_x_T[:],
+            in0=x_T[:].rearrange("p m (b l) -> p m b l", l=L),
+            in1=shift[:].unsqueeze(2).to_broadcast([P, CHUNKS, B, L]),
+        )
         gain_ps = psum.tile([ROWS, C], F32)
-        shift_ps = psum.tile([ROWS, C], F32)
         for m in range(CHUNKS):
-            nc.tensor.transpose(gain_ps[:, m * P : (m + 1) * P], gain_rep[:, m, :], ident_f32[:])
+            nc.tensor.matmul(
+                out=gain_ps[:, m * P : (m + 1) * P],
+                lhsT=gain[:, m : m + 1].to_broadcast([P, ROWS]),
+                rhs=ident_f32[:],
+                start=True,
+                stop=True,
+            )
+        shift_x_ps = psum.tile([ROWS, C], F32)
         for m in range(CHUNKS):
             nc.tensor.transpose(
-                shift_ps[:, m * P : (m + 1) * P], shift_rep[:, m].rearrange("p b l -> p (b l)"), ident_f32[:]
+                shift_x_ps[:, m * P : (m + 1) * P], shift_x_T[:, m].rearrange("p b l -> p (b l)"), ident_f32[:]
             )
+
+        regroup_piece(1)
         gain_rows = keep.tile([ROWS, C], F32)
         nc.scalar.copy(out=gain_rows[:], in_=gain_ps[:])
-        shift_x = keep.tile([ROWS, C], F32)
-        nc.vector.tensor_add(out=shift_x[:], in0=shift_ps[:], in1=x_rows[:])
+        quantise_and_multiply_piece(0)
 
-        last = len(kernels) - 1
-        pieces = [(m, 0, C) for m in range(last)] + [(last, 0, HALF), (last, HALF, HALF)]
-        y_ps = [psum.tile([ROWS, HALF], F32, name="y_ps%d" % half) for half in range(2)]
-        w_codes = [keep.tile([P, C], U32, name="w_codes%d" % m, align_bytes=64) for m in range(len(kernels))]
-        w_scales = [keep.tile([P, C], U8, name="w_scales%d" % m, align_bytes=64) for m in range(len(kernels))]
-        for m, first, width in pieces:
-            i, l = kernels[m]
-            vector_cols = width * VECTOR_SHARE[0] // VECTOR_SHARE[1]
-            grouped = stage.tile([P, C, PACK], BF16, align_bytes=64)
-            regroup(nc.vector.tensor_copy, grouped, w_raw[m], slice(first, first + vector_cols))
-            regroup(nc.scalar.copy, grouped, w_raw[m], slice(first + vector_cols, first + width))
-            cols = slice(first, first + width)
-            nc.vector.quantize_mx(
-                out=w_codes[m][:, cols].bitcast(FP8X4),
-                scales=w_scales[m][:, cols],
-                in_=grouped[:, cols, :].rearrange("p f t -> p (f t)"),
-            )
-            source = (l - STEPS[i]) % L
-            operand = slice((l * L + source) * ROWS, (l * L + source + 1) * ROWS)
-            for half in range(first // HALF, (first + width) // HALF):
-                half_cols = slice(half * HALF, (half + 1) * HALF)
-                nc.tensor.matmul_mx(
-                    out=y_ps[half][:],
-                    lhsT=h_codes[:, operand].bitcast(FP8X4),
-                    lhsT_scale=h_scales[:, operand],
-                    rhs=w_codes[m][:, half_cols].bitcast(FP8X4),
-                    rhs_scale=w_scales[m][:, half_cols],
-                    start=(m == 0),
-                    stop=(m == last),
-                )
+        for j in range(2, len(pieces)):
+            regroup_piece(j)
+            quantise_and_multiply_piece(j - 1)
+        quantise_and_multiply_piece(len(pieces) - 1)
 
         out_rows = out.rearrange("b l f -> (b l) f")
-        for half in range(2):
-            cols = slice(half * HALF, (half + 1) * HALF)
-            gy = stage.tile([ROWS, HALF], F32)
-            nc.vector.tensor_mul(out=gy[:], in0=y_ps[half][:], in1=gain_rows[:, cols])
-            z = stage.tile([ROWS, HALF], F32)
-            nc.vector.tensor_add(out=z[:], in0=gy[:], in1=shift_x[:, cols])
-            res = stage.tile([ROWS, HALF], F32)
+        for g, (first, width) in enumerate(GROUPS):
+            cols = slice(first, first + width)
+            gy = keep.tile([ROWS, width], F32, name="gy%d" % g)
+            nc.vector.tensor_mul(out=gy[:], in0=y_ps[g][:], in1=gain_rows[:, cols])
+            z = keep.tile([ROWS, width], F32, name="z%d" % g)
+            nc.vector.tensor_add(out=z[:], in0=gy[:], in1=shift_x_ps[:, cols])
+            res = keep.tile([ROWS, width], F32, name="res%d" % g)
             nc.vector.scalar_tensor_tensor(
                 out=res[:], in0=z[:], scalar=LEAKY_ALPHA, in1=z[:], op0=ALU.mult, op1=ALU.max
             )

@@ -19,7 +19,7 @@ CHUNKS = C // P
 BN_EPS = 1e-3
 LEAKY_ALPHA = 0.3
 RUN = 4
-VECTOR_SHARE = (7, 16)
+VECTOR_SHARE = (1, 2)
 GROUPS = ((0, C // 2), (C // 2, C // 4), (3 * C // 4, C // 4))
 
 FLOPS = 2 * B * L * TAPS * C * C

@@ -68,21 +68,18 @@ def tile_residualblock5_pb_s_kernel(tc, h, x, k2, b2, gamma2, beta2, mean2, var2
         make_identity(nc, ident_bf16[:])
 
         h_words = h_rows[:].bitcast(F32).rearrange("r (p u) -> r u p", u=2)
-        h_grouped = keep.tile([P, L * L * ROWS * PACK], BF16, align_bytes=64)
-        nc.vector.memset(h_grouped[:], 0.0)
-        h_grouped_words = h_grouped[:].bitcast(F32).rearrange(
-            "p (o s b l u) -> p o s b l u", o=L, s=L, b=B, l=L, u=2
-        )
+        h_codes = keep.tile([P, (2 * L + 1) * B], U32, align_bytes=64)
+        h_scales = keep.tile([P, (2 * L + 1) * B], U8, align_bytes=64)
+        nc.vector.memset(h_codes[:].rearrange("p (g b) -> p g b", b=B)[:, 0::2, :], 0)
+        nc.vector.memset(h_scales[:].bitcast(U32).rearrange("p (g b) -> p g b", b=B // PACK)[:, 0::2, :], 0)
         h_T = psum.tile([P, 2, ROWS], F32)
         for u in range(2):
             nc.tensor.transpose(h_T[:, u, :], h_words[:, u, :], ident_f32[:])
-        for o in range(L):
-            nc.scalar.copy(
-                out=h_grouped_words[:, o, :, :, o, :],
-                in_=h_T[:].rearrange("p u (b s) -> p s b u", s=L),
-            )
-        h_codes = keep.tile([P, L * L * ROWS], U32, align_bytes=64)
-        h_scales = keep.tile([P, L * L * ROWS], U8, align_bytes=64)
+        h_grouped = keep.tile([P, L, B * PACK], BF16, align_bytes=64)
+        nc.scalar.copy(
+            out=h_grouped[:].rearrange("p s w -> p (s w)").bitcast(F32).rearrange("p (s b u) -> p s b u", s=L, u=2),
+            in_=h_T[:].rearrange("p u (b s) -> p s b u", s=L),
+        )
 
         params_T = psum.tile([P, CHUNKS, P], BF16)
         for m in range(CHUNKS):
@@ -120,7 +117,8 @@ def tile_residualblock5_pb_s_kernel(tc, h, x, k2, b2, gamma2, beta2, mean2, var2
                 in_=grouped_of[j][:, cols, :].rearrange("p f t -> p (f t)"),
             )
             source = (l - STEPS[i]) % L
-            operand = slice((l * L + source) * ROWS, (l * L + source + 1) * ROWS)
+            operand_first = (2 * source + 1 - l) * B
+            operand = slice(operand_first, operand_first + ROWS)
             for g, (group_first, group_width) in enumerate(GROUPS):
                 if first <= group_first < first + width:
                     group_cols = slice(group_first, group_first + group_width)
@@ -159,13 +157,17 @@ def tile_residualblock5_pb_s_kernel(tc, h, x, k2, b2, gamma2, beta2, mean2, var2
         shift = keep.tile([P, CHUNKS, L], F32)
         nc.vector.tensor_add(out=shift[:], in0=scaled[:], in1=beta_c.unsqueeze(2).to_broadcast([P, CHUNKS, L]))
 
-        nc.vector.quantize_mx(out=h_codes[:].bitcast(FP8X4), scales=h_scales[:], in_=h_grouped[:])
+        for source in range(L):
+            live = slice((2 * source + 1) * B, (2 * source + 2) * B)
+            nc.vector.quantize_mx(
+                out=h_codes[:, live].bitcast(FP8X4), scales=h_scales[:, live], in_=h_grouped[:, source, :]
+            )
 
-        shift_x_T = keep.tile([P, CHUNKS, B, L], F32)
+        shift_x_T = keep.tile([P, CHUNKS, L, B], F32)
         nc.vector.tensor_add(
             out=shift_x_T[:],
-            in0=x_T[:].rearrange("p m (b l) -> p m b l", l=L),
-            in1=shift[:].unsqueeze(2).to_broadcast([P, CHUNKS, B, L]),
+            in0=x_T[:].rearrange("p m (b l) -> p m l b", l=L),
+            in1=shift[:].unsqueeze(3).to_broadcast([P, CHUNKS, L, B]),
         )
         gain_ps = psum.tile([ROWS, C], F32)
         for m in range(CHUNKS):
@@ -179,7 +181,7 @@ def tile_residualblock5_pb_s_kernel(tc, h, x, k2, b2, gamma2, beta2, mean2, var2
         shift_x_ps = psum.tile([ROWS, C], F32)
         for m in range(CHUNKS):
             nc.tensor.transpose(
-                shift_x_ps[:, m * P : (m + 1) * P], shift_x_T[:, m].rearrange("p b l -> p (b l)"), ident_f32[:]
+                shift_x_ps[:, m * P : (m + 1) * P], shift_x_T[:, m].rearrange("p l b -> p (l b)"), ident_f32[:]
             )
 
         regroup_piece(1)
@@ -192,7 +194,6 @@ def tile_residualblock5_pb_s_kernel(tc, h, x, k2, b2, gamma2, beta2, mean2, var2
             quantise_and_multiply_piece(j - 1)
         quantise_and_multiply_piece(len(pieces) - 1)
 
-        out_rows = out.rearrange("b l f -> (b l) f")
         for g, (first, width) in enumerate(GROUPS):
             cols = slice(first, first + width)
             gy = keep.tile([ROWS, width], F32, name="gy%d" % g)
@@ -203,4 +204,5 @@ def tile_residualblock5_pb_s_kernel(tc, h, x, k2, b2, gamma2, beta2, mean2, var2
             nc.vector.scalar_tensor_tensor(
                 out=res[:], in0=z[:], scalar=LEAKY_ALPHA, in1=z[:], op0=ALU.mult, op1=ALU.max
             )
-            nc.sync.dma_start(out=out_rows[:, cols], in_=res[:])
+            for l, queue in enumerate((nc.sync, nc.scalar)):
+                queue.dma_start(out=out[:, l, cols], in_=res[l * B : (l + 1) * B, :])

@@ -9,6 +9,7 @@ U32 = mybir.dt.uint32
 U8 = mybir.dt.uint8
 FP8X4 = mybir.dt.float8_e4m3fn_x4
 ALU = mybir.AluOpType
+ACT = mybir.ActivationFunctionType
 
 P = 128
 PACK = 4
@@ -19,7 +20,7 @@ CHUNKS = C // P
 BN_EPS = 1e-3
 LEAKY_ALPHA = 0.3
 RUN = 4
-VECTOR_SHARE = (1, 2)
+VECTOR_COLS = {512: 256, 256: 96, 128: 48}
 GROUPS = ((0, C // 2), (C // 2, C // 4), (3 * C // 4, C // 4))
 
 FLOPS = 2 * B * L * TAPS * C * C
@@ -38,29 +39,36 @@ def tile_residualblock5_pb_s_kernel(tc, h, x, k2, b2, gamma2, beta2, mean2, var2
         keep = ctx.enter_context(tc.tile_pool(name="keep", bufs=1))
         stage = ctx.enter_context(tc.tile_pool(name="stage", bufs=4))
         psum = ctx.enter_context(tc.psum_pool(name="psum", bufs=1))
+        ctx.enter_context(tc.manual_schedule())
 
         one = keep.tile([P, 1], F32)
         nc.vector.memset(one[:], 1.0)
         warm = keep.tile([P, 1], F32)
-        nc.scalar.sqrt(out=warm[:], in_=one[:])
-
-        h_rows = keep.tile([ROWS, C], BF16)
-        nc.sync.dma_start(out=h_rows[:], in_=h.rearrange("b l c -> (b l) c"))
+        nc.scalar.activation(out=warm[:], in_=one[:], func=ACT.Abs_reciprocal_sqrt)
 
         params = keep.tile([P, C], BF16)
         nc.vector.memset(params[:], 0.0)
-        for row, vec in enumerate((gamma2, beta2, mean2, var2)):
-            nc.scalar.dma_start(out=params[row : row + 1, :], in_=vec.unsqueeze(0))
-        nc.scalar.dma_start(out=params[4:6, :], in_=b2)
+        h_rows = keep.tile([ROWS, C], BF16)
         x_rows = keep.tile([ROWS, C], BF16)
-        nc.scalar.dma_start(out=x_rows[:], in_=x.rearrange("b l c -> (b l) c"))
-
         kernels = [(i, l) for i in range(TAPS) for l in range(L)]
         w_raw = []
-        for m, (i, l) in enumerate(kernels):
-            raw = keep.tile([P, PACK, C], BF16, name="w_raw%d" % m)
+
+        def load_kernel():
+            i, l = kernels[len(w_raw)]
+            raw = keep.tile([P, PACK, C], BF16, name="w_raw%d" % len(w_raw))
             nc.sync.dma_start(out=raw[:], in_=k2[i, l].rearrange("(p t) f -> p t f", t=PACK))
             w_raw.append(raw)
+
+        nc.sync.dma_start(out=h_rows[:], in_=h.rearrange("b l c -> (b l) c"))
+        load_kernel()
+        for row, vec in enumerate((gamma2, beta2, mean2, var2)):
+            nc.sync.dma_start(out=params[row : row + 1, :], in_=vec.unsqueeze(0))
+        nc.sync.dma_start(out=params[4:6, :], in_=b2)
+        for m in range(1, 4):
+            load_kernel()
+        nc.sync.dma_start(out=x_rows[:], in_=x.rearrange("b l c -> (b l) c"))
+        for m in range(4, len(kernels)):
+            load_kernel()
 
         ident_f32 = keep.tile([P, P], F32)
         make_identity(nc, ident_f32[:])
@@ -73,136 +81,170 @@ def tile_residualblock5_pb_s_kernel(tc, h, x, k2, b2, gamma2, beta2, mean2, var2
         nc.vector.memset(h_codes[:].rearrange("p (g b) -> p g b", b=B)[:, 0::2, :], 0)
         nc.vector.memset(h_scales[:].bitcast(U32).rearrange("p (g b) -> p g b", b=B // PACK)[:, 0::2, :], 0)
         h_T = psum.tile([P, 2, ROWS], F32)
-        for u in range(2):
-            nc.tensor.transpose(h_T[:, u, :], h_words[:, u, :], ident_f32[:])
         h_grouped = keep.tile([P, L, B * PACK], BF16, align_bytes=64)
-        nc.scalar.copy(
-            out=h_grouped[:].rearrange("p s w -> p (s w)").bitcast(F32).rearrange("p (s b u) -> p s b u", s=L, u=2),
-            in_=h_T[:].rearrange("p u (b s) -> p s b u", s=L),
-        )
 
-        params_T = psum.tile([P, CHUNKS, P], BF16)
-        for m in range(CHUNKS):
-            nc.tensor.transpose(params_T[:, m, :], params[:, m * P : (m + 1) * P], ident_bf16[:])
-        x_T = psum.tile([P, CHUNKS, ROWS], BF16)
-        for m in range(CHUNKS):
-            nc.tensor.transpose(x_T[:, m, :], x_rows[:, m * P : (m + 1) * P], ident_bf16[:])
-        pvals = keep.tile([P, 6, CHUNKS], F32)
-        nc.vector.tensor_copy(out=pvals[:], in_=params_T[:, :, 0:6].rearrange("p m v -> p v m"))
-        gamma_c, beta_c, mean_c, var_c = pvals[:, 0, :], pvals[:, 1, :], pvals[:, 2, :], pvals[:, 3, :]
-        b2_c = pvals[:, 4:6, :].rearrange("p l m -> p m l")
+        def transpose_h():
+            for u in range(2):
+                nc.tensor.transpose(h_T[:, u, :], h_words[:, u, :], ident_f32[:])
+
+        def copy_h():
+            nc.scalar.copy(
+                out=h_grouped[:].rearrange("p s w -> p (s w)").bitcast(F32).rearrange("p (s b u) -> p s b u", s=L, u=2),
+                in_=h_T[:].rearrange("p u (b s) -> p s b u", s=L),
+            )
+
+        def quantise_h():
+            for source in range(L):
+                live = slice((2 * source + 1) * B, (2 * source + 2) * B)
+                nc.vector.quantize_mx(
+                    out=h_codes[:, live].bitcast(FP8X4), scales=h_scales[:, live], in_=h_grouped[:, source, :]
+                )
 
         last = len(kernels) - 1
         pieces = [(m, 0, C) for m in range(last)] + [(last, first, width) for first, width in GROUPS]
-        y_ps = [psum.tile([ROWS, width], F32, name="y_ps%d" % g) for g, (first, width) in enumerate(GROUPS)]
+        y_ps = [psum.tile([P, ROWS], F32, name="y_ps%d" % c) for c in range(CHUNKS)]
         w_codes = [keep.tile([P, C], U32, name="w_codes%d" % m, align_bytes=64) for m in range(len(kernels))]
         w_scales = [keep.tile([P, C], U8, name="w_scales%d" % m, align_bytes=64) for m in range(len(kernels))]
         grouped_of = {}
 
         def regroup_piece(j):
             m, first, width = pieces[j]
-            vector_cols = width * VECTOR_SHARE[0] // VECTOR_SHARE[1]
+            vector_cols = VECTOR_COLS[width]
             grouped = stage.tile([P, C, PACK], BF16, align_bytes=64)
             regroup(nc.vector.tensor_copy, grouped, w_raw[m], slice(first, first + vector_cols))
             regroup(nc.scalar.copy, grouped, w_raw[m], slice(first + vector_cols, first + width))
             grouped_of[j] = grouped
 
-        def quantise_and_multiply_piece(j):
+        def quantise_piece(j):
             m, first, width = pieces[j]
-            i, l = kernels[m]
             cols = slice(first, first + width)
             nc.vector.quantize_mx(
                 out=w_codes[m][:, cols].bitcast(FP8X4),
                 scales=w_scales[m][:, cols],
                 in_=grouped_of[j][:, cols, :].rearrange("p f t -> p (f t)"),
             )
+
+        def multiply_piece(j):
+            m, first, width = pieces[j]
+            i, l = kernels[m]
             source = (l - STEPS[i]) % L
             operand_first = (2 * source + 1 - l) * B
             operand = slice(operand_first, operand_first + ROWS)
-            for g, (group_first, group_width) in enumerate(GROUPS):
-                if first <= group_first < first + width:
-                    group_cols = slice(group_first, group_first + group_width)
-                    nc.tensor.matmul_mx(
-                        out=y_ps[g][:],
-                        lhsT=h_codes[:, operand].bitcast(FP8X4),
-                        lhsT_scale=h_scales[:, operand],
-                        rhs=w_codes[m][:, group_cols].bitcast(FP8X4),
-                        rhs_scale=w_scales[m][:, group_cols],
-                        start=(m == 0),
-                        stop=(m == last),
-                    )
+            for c in range(first // P, (first + width) // P):
+                chunk = slice(c * P, (c + 1) * P)
+                nc.tensor.matmul_mx(
+                    out=y_ps[c][:],
+                    lhsT=w_codes[m][:, chunk].bitcast(FP8X4),
+                    lhsT_scale=w_scales[m][:, chunk],
+                    rhs=h_codes[:, operand].bitcast(FP8X4),
+                    rhs_scale=h_scales[:, operand],
+                    start=(m == 0),
+                    stop=(m == last),
+                )
 
-        var_eps = keep.tile([P, CHUNKS], F32)
-        nc.vector.tensor_scalar_add(out=var_eps[:], in0=var_c, scalar1=BN_EPS)
-        std = keep.tile([P, CHUNKS], F32)
-        nc.scalar.sqrt(out=std[:], in_=var_eps[:])
-        centred = keep.tile([P, CHUNKS, L], F32)
-        nc.vector.scalar_tensor_tensor(
-            out=centred[:],
-            in0=b2_c,
-            scalar=2.0,
-            in1=mean_c.unsqueeze(2).to_broadcast([P, CHUNKS, L]),
-            op0=ALU.mult,
-            op1=ALU.subtract,
-        )
-
-        regroup_piece(0)
-
+        params_T = psum.tile([P, CHUNKS, P], BF16)
+        x_T = psum.tile([P, CHUNKS, ROWS], BF16)
+        pvals = keep.tile([P, 6, CHUNKS], F32)
+        gamma_c, beta_c, mean_c, var_c = pvals[:, 0, :], pvals[:, 1, :], pvals[:, 2, :], pvals[:, 3, :]
+        b2_c = pvals[:, 4:6, :].rearrange("p l m -> p m l")
         rstd = keep.tile([P, CHUNKS], F32)
-        nc.vector.reciprocal(out=rstd[:], in_=std[:])
+        centred = keep.tile([P, CHUNKS, L], F32)
         gain = keep.tile([P, CHUNKS], F32)
-        nc.vector.tensor_mul(out=gain[:], in0=gamma_c, in1=rstd[:])
         scaled = keep.tile([P, CHUNKS, L], F32)
-        nc.vector.tensor_mul(out=scaled[:], in0=centred[:], in1=gain[:].unsqueeze(2).to_broadcast([P, CHUNKS, L]))
         shift = keep.tile([P, CHUNKS, L], F32)
-        nc.vector.tensor_add(out=shift[:], in0=scaled[:], in1=beta_c.unsqueeze(2).to_broadcast([P, CHUNKS, L]))
+        shift_x = keep.tile([P, CHUNKS, ROWS], F32)
 
-        for source in range(L):
-            live = slice((2 * source + 1) * B, (2 * source + 2) * B)
-            nc.vector.quantize_mx(
-                out=h_codes[:, live].bitcast(FP8X4), scales=h_scales[:, live], in_=h_grouped[:, source, :]
-            )
+        def transpose_params():
+            for m in range(CHUNKS):
+                nc.tensor.transpose(params_T[:, m, :], params[:, m * P : (m + 1) * P], ident_bf16[:])
 
-        shift_x_T = keep.tile([P, CHUNKS, L, B], F32)
-        nc.vector.tensor_add(
-            out=shift_x_T[:],
-            in0=x_T[:].rearrange("p m (b l) -> p m l b", l=L),
-            in1=shift[:].unsqueeze(3).to_broadcast([P, CHUNKS, L, B]),
-        )
-        gain_ps = psum.tile([ROWS, C], F32)
-        for m in range(CHUNKS):
-            nc.tensor.matmul(
-                out=gain_ps[:, m * P : (m + 1) * P],
-                lhsT=gain[:, m : m + 1].to_broadcast([P, ROWS]),
-                rhs=ident_f32[:],
-                start=True,
-                stop=True,
-            )
-        shift_x_ps = psum.tile([ROWS, C], F32)
-        for m in range(CHUNKS):
-            nc.tensor.transpose(
-                shift_x_ps[:, m * P : (m + 1) * P], shift_x_T[:, m].rearrange("p l b -> p (l b)"), ident_f32[:]
-            )
+        def copy_params():
+            nc.scalar.copy(out=pvals[:], in_=params_T[:, :, 0:6].rearrange("p m v -> p v m"))
 
-        regroup_piece(1)
-        gain_rows = keep.tile([ROWS, C], F32)
-        nc.scalar.copy(out=gain_rows[:], in_=gain_ps[:])
-        quantise_and_multiply_piece(0)
+        def take_rstd():
+            nc.scalar.activation(out=rstd[:], in_=var_c, func=ACT.Abs_reciprocal_sqrt, bias=BN_EPS)
 
-        for j in range(2, len(pieces)):
-            regroup_piece(j)
-            quantise_and_multiply_piece(j - 1)
-        quantise_and_multiply_piece(len(pieces) - 1)
-
-        for g, (first, width) in enumerate(GROUPS):
-            cols = slice(first, first + width)
-            gy = keep.tile([ROWS, width], F32, name="gy%d" % g)
-            nc.vector.tensor_mul(out=gy[:], in0=y_ps[g][:], in1=gain_rows[:, cols])
-            z = keep.tile([ROWS, width], F32, name="z%d" % g)
-            nc.vector.tensor_add(out=z[:], in0=gy[:], in1=shift_x_ps[:, cols])
-            res = keep.tile([ROWS, width], F32, name="res%d" % g)
+        def take_gain():
             nc.vector.scalar_tensor_tensor(
-                out=res[:], in0=z[:], scalar=LEAKY_ALPHA, in1=z[:], op0=ALU.mult, op1=ALU.max
+                out=centred[:],
+                in0=b2_c,
+                scalar=2.0,
+                in1=mean_c.unsqueeze(2).to_broadcast([P, CHUNKS, L]),
+                op0=ALU.mult,
+                op1=ALU.subtract,
             )
-            for l, queue in enumerate((nc.sync, nc.scalar)):
-                queue.dma_start(out=out[:, l, cols], in_=res[l * B : (l + 1) * B, :])
+            nc.vector.tensor_mul(out=gain[:], in0=gamma_c, in1=rstd[:])
+
+        def scale_shift():
+            nc.vector.tensor_mul(out=scaled[:], in0=centred[:], in1=gain[:].unsqueeze(2).to_broadcast([P, CHUNKS, L]))
+
+        def take_shift():
+            nc.vector.tensor_add(out=shift[:], in0=scaled[:], in1=beta_c.unsqueeze(2).to_broadcast([P, CHUNKS, L]))
+
+        def transpose_x():
+            for m in range(CHUNKS):
+                nc.tensor.transpose(x_T[:, m, :], x_rows[:, m * P : (m + 1) * P], ident_bf16[:])
+
+        def add_shift(m):
+            for l in range(L):
+                nc.scalar.activation(
+                    out=shift_x[:, m, l * B : (l + 1) * B],
+                    in_=x_T[:, m, :].rearrange("p (b l) -> p l b", l=L)[:, l, :],
+                    func=ACT.Identity,
+                    bias=shift[:, m, l : l + 1],
+                )
+
+        z = [keep.tile([P, width], F32, name="z%d" % g) for g, (first, width) in enumerate(GROUPS)]
+        res_T = [keep.tile([P, width], F32, name="res_T%d" % g) for g, (first, width) in enumerate(GROUPS)]
+
+        def take_z(g):
+            first, width = GROUPS[g]
+            for k in range(width // P):
+                c = first // P + k
+                nc.vector.scalar_tensor_tensor(
+                    out=z[g][:, k * P : (k + 1) * P],
+                    in0=y_ps[c][:],
+                    scalar=gain[:, c : c + 1],
+                    in1=shift_x[:, c, :],
+                    op0=ALU.mult,
+                    op1=ALU.add,
+                )
+
+        def finish(g):
+            first, width = GROUPS[g]
+            nc.vector.scalar_tensor_tensor(
+                out=res_T[g][:], in0=z[g][:], scalar=LEAKY_ALPHA, in1=z[g][:], op0=ALU.mult, op1=ALU.max
+            )
+            back = psum.tile([ROWS, width], F32, name="back%d" % g, tag=("h_T", "params_T", "x_T")[g])
+            for k in range(width // P):
+                cols = slice(k * P, (k + 1) * P)
+                nc.tensor.transpose(back[:, cols], res_T[g][:, cols], ident_f32[:])
+            res = keep.tile([ROWS, width], F32, name="res%d" % g)
+            nc.scalar.copy(out=res[:], in_=back[:])
+            for l in range(L):
+                nc.sync.dma_start(out=out[:, l, first : first + width], in_=res[l * B : (l + 1) * B, :])
+
+        after_regroup = {
+            0: (transpose_h, transpose_params, copy_params),
+            1: (take_rstd, copy_h),
+            6: (lambda: add_shift(0), lambda: add_shift(1)),
+            7: (lambda: add_shift(2), lambda: add_shift(3)),
+        }
+        after_quantise = {0: (quantise_h, take_gain), 1: (scale_shift,), 2: (take_shift,), 4: (transpose_x,)}
+
+        for j in range(len(pieces) + 1):
+            if j < len(pieces):
+                regroup_piece(j)
+                for step in after_regroup.get(j, ()):
+                    step()
+            if j > 0:
+                quantise_piece(j - 1)
+                for step in after_quantise.get(j - 1, ()):
+                    step()
+                multiply_piece(j - 1)
+        take_z(0)
+        take_z(1)
+        finish(0)
+        take_z(2)
+        finish(1)
+        finish(2)

@@ -15,6 +15,7 @@ P = 128
 PACK = 4
 B, L, C, TAPS = 64, 2, 512, 5
 ROWS = B * L
+THROUGH_TENSOR = 2 * TAPS - 2
 STEPS = (0, 0, 1, -1, 2)
 CHUNKS = C // P
 BN_EPS = 1e-3
@@ -112,7 +113,19 @@ def tile_residualblock5_pb_s_kernel(tc, h, x, k2, b2, gamma2, beta2, mean2, var2
             vector_cols = VECTOR_COLS[width]
             grouped = stage.tile([P, C, PACK], BF16, align_bytes=64)
             regroup(nc.vector.tensor_copy, grouped, w_raw[m], slice(first, first + vector_cols))
-            regroup(nc.scalar.copy, grouped, w_raw[m], slice(first + vector_cols, first + width))
+            if m == THROUGH_TENSOR:
+                moved = psum.tile([P, C - vector_cols, PACK], BF16, tag="params_T")
+                for f in range(0, C - vector_cols, P):
+                    nc.tensor.matmul(
+                        out=moved[:, f : f + P, :].rearrange("p f t -> p (f t)"),
+                        lhsT=ident_bf16[:],
+                        rhs=w_raw[m][:, :, vector_cols + f : vector_cols + f + P].rearrange("p t f -> p f t"),
+                        start=True,
+                        stop=True,
+                    )
+                nc.scalar.copy(out=grouped[:, vector_cols:, :], in_=moved[:])
+            else:
+                regroup(nc.scalar.copy, grouped, w_raw[m], slice(first + vector_cols, first + width))
             grouped_of[j] = grouped
 
         def quantise_piece(j):

@@ -15,7 +15,7 @@ P = 128
 PACK = 4
 B, L, C, TAPS = 64, 2, 512, 5
 ROWS = B * L
-THROUGH_TENSOR = 2 * TAPS - 2
+THROUGH_TENSOR = 8
 STEPS = (0, 0, 1, -1, 2)
 CHUNKS = C // P
 BN_EPS = 1e-3
@@ -107,6 +107,7 @@ def tile_residualblock5_pb_s_kernel(tc, h, x, k2, b2, gamma2, beta2, mean2, var2
         w_codes = [keep.tile([P, C], U32, name="w_codes%d" % m, align_bytes=64) for m in range(len(kernels))]
         w_scales = [keep.tile([P, C], U8, name="w_scales%d" % m, align_bytes=64) for m in range(len(kernels))]
         grouped_of = {}
+        moved_of = {}
 
         def regroup_piece(j):
             m, first, width = pieces[j]
@@ -114,19 +115,23 @@ def tile_residualblock5_pb_s_kernel(tc, h, x, k2, b2, gamma2, beta2, mean2, var2
             grouped = stage.tile([P, C, PACK], BF16, align_bytes=64)
             regroup(nc.vector.tensor_copy, grouped, w_raw[m], slice(first, first + vector_cols))
             if m == THROUGH_TENSOR:
-                moved = psum.tile([P, C - vector_cols, PACK], BF16, tag="params_T")
-                for f in range(0, C - vector_cols, P):
-                    nc.tensor.matmul(
-                        out=moved[:, f : f + P, :].rearrange("p f t -> p (f t)"),
-                        lhsT=ident_bf16[:],
-                        rhs=w_raw[m][:, :, vector_cols + f : vector_cols + f + P].rearrange("p t f -> p f t"),
-                        start=True,
-                        stop=True,
-                    )
-                nc.scalar.copy(out=grouped[:, vector_cols:, :], in_=moved[:])
+                nc.scalar.copy(out=grouped[:, vector_cols:, :], in_=moved_of[m][:])
             else:
                 regroup(nc.scalar.copy, grouped, w_raw[m], slice(first + vector_cols, first + width))
             grouped_of[j] = grouped
+
+        def move_through_tensor():
+            first = VECTOR_COLS[C]
+            moved = psum.tile([P, C - first, PACK], BF16, tag="params_T")
+            for f in range(0, C - first, P):
+                nc.tensor.matmul(
+                    out=moved[:, f : f + P, :].rearrange("p f t -> p (f t)"),
+                    lhsT=ident_bf16[:],
+                    rhs=w_raw[THROUGH_TENSOR][:, :, first + f : first + f + P].rearrange("p t f -> p f t"),
+                    start=True,
+                    stop=True,
+                )
+            moved_of[THROUGH_TENSOR] = moved
 
         def quantise_piece(j):
             m, first, width = pieces[j]
@@ -243,7 +248,13 @@ def tile_residualblock5_pb_s_kernel(tc, h, x, k2, b2, gamma2, beta2, mean2, var2
             6: (lambda: add_shift(0), lambda: add_shift(1)),
             7: (lambda: add_shift(2), lambda: add_shift(3)),
         }
-        after_quantise = {0: (quantise_h, take_gain), 1: (scale_shift,), 2: (take_shift,), 4: (transpose_x,)}
+        after_quantise = {
+            0: (quantise_h, take_gain),
+            1: (scale_shift,),
+            2: (take_shift,),
+            4: (transpose_x,),
+            5: (move_through_tensor,),
+        }
 
         for j in range(len(pieces) + 1):
             if j < len(pieces):

@@ -16,12 +16,14 @@ PACK = 4
 B, L, C, TAPS = 64, 2, 512, 5
 ROWS = B * L
 THROUGH_TENSOR = 8
+MOVED = 128
 STEPS = (0, 0, 1, -1, 2)
 CHUNKS = C // P
 BN_EPS = 1e-3
 LEAKY_ALPHA = 0.3
 RUN = 4
-VECTOR_COLS = {512: 256, 256: 96, 128: 48}
+VECTOR_COLS = {512: 248, 256: 96, 128: 48}
+VECTOR_COLS_FIRST = 336
 GROUPS = ((0, C // 2), (C // 2, C // 4), (3 * C // 4, C // 4))
 
 FLOPS = 2 * B * L * TAPS * C * C
@@ -47,7 +49,7 @@ def tile_residualblock5_pb_s_kernel(tc, h, x, k2, b2, gamma2, beta2, mean2, var2
         warm = keep.tile([P, 1], F32)
         nc.scalar.activation(out=warm[:], in_=one[:], func=ACT.Abs_reciprocal_sqrt)
 
-        params = keep.tile([P, C], BF16)
+        params = keep.tile([P, P], BF16)
         nc.vector.memset(params[:], 0.0)
         h_rows = keep.tile([ROWS, C], BF16)
         x_rows = keep.tile([ROWS, C], BF16)
@@ -62,14 +64,15 @@ def tile_residualblock5_pb_s_kernel(tc, h, x, k2, b2, gamma2, beta2, mean2, var2
 
         nc.sync.dma_start(out=h_rows[:], in_=h.rearrange("b l c -> (b l) c"))
         load_kernel()
-        for row, vec in enumerate((gamma2, beta2, mean2, var2)):
-            nc.sync.dma_start(out=params[row : row + 1, :], in_=vec.unsqueeze(0))
-        nc.sync.dma_start(out=params[4:6, :], in_=b2)
+        for v, vec in enumerate((gamma2, beta2, mean2, var2)):
+            nc.sync.dma_start(out=params[v * CHUNKS : (v + 1) * CHUNKS, :], in_=vec.rearrange("(m p) -> m p", p=P))
+        nc.sync.dma_start(out=params[4 * CHUNKS : 6 * CHUNKS, :], in_=b2.rearrange("l (m p) -> (l m) p", p=P))
         for m in range(1, 4):
             load_kernel()
-        nc.sync.dma_start(out=x_rows[:], in_=x.rearrange("b l c -> (b l) c"))
         for m in range(4, len(kernels)):
             load_kernel()
+        for l in range(L):
+            nc.sync.dma_start(out=x_rows[l * B : (l + 1) * B, :], in_=x[:, l, :])
 
         ident_f32 = keep.tile([P, P], F32)
         make_identity(nc, ident_f32[:])
@@ -111,19 +114,20 @@ def tile_residualblock5_pb_s_kernel(tc, h, x, k2, b2, gamma2, beta2, mean2, var2
 
         def regroup_piece(j):
             m, first, width = pieces[j]
-            vector_cols = VECTOR_COLS[width]
+            vector_cols = VECTOR_COLS_FIRST if j == 0 else VECTOR_COLS[width]
             grouped = stage.tile([P, C, PACK], BF16, align_bytes=64)
             regroup(nc.vector.tensor_copy, grouped, w_raw[m], slice(first, first + vector_cols))
+            scalar_first = first + vector_cols
             if m == THROUGH_TENSOR:
-                nc.scalar.copy(out=grouped[:, vector_cols:, :], in_=moved_of[m][:])
-            else:
-                regroup(nc.scalar.copy, grouped, w_raw[m], slice(first + vector_cols, first + width))
+                nc.scalar.copy(out=grouped[:, scalar_first : scalar_first + MOVED, :], in_=moved_of[m][:])
+                scalar_first += MOVED
+            regroup(nc.scalar.copy, grouped, w_raw[m], slice(scalar_first, first + width))
             grouped_of[j] = grouped
 
         def move_through_tensor():
             first = VECTOR_COLS[C]
-            moved = psum.tile([P, C - first, PACK], BF16, tag="params_T")
-            for f in range(0, C - first, P):
+            moved = psum.tile([P, MOVED, PACK], BF16)
+            for f in range(0, MOVED, P):
                 nc.tensor.matmul(
                     out=moved[:, f : f + P, :].rearrange("p f t -> p (f t)"),
                     lhsT=ident_bf16[:],
@@ -160,8 +164,7 @@ def tile_residualblock5_pb_s_kernel(tc, h, x, k2, b2, gamma2, beta2, mean2, var2
                     stop=(m == last),
                 )
 
-        params_T = psum.tile([P, CHUNKS, P], BF16)
-        x_T = psum.tile([P, CHUNKS, ROWS], BF16)
+        params_T = psum.tile([P, P], BF16)
         pvals = keep.tile([P, 6, CHUNKS], F32)
         gamma_c, beta_c, mean_c, var_c = pvals[:, 0, :], pvals[:, 1, :], pvals[:, 2, :], pvals[:, 3, :]
         b2_c = pvals[:, 4:6, :].rearrange("p l m -> p m l")
@@ -170,14 +173,12 @@ def tile_residualblock5_pb_s_kernel(tc, h, x, k2, b2, gamma2, beta2, mean2, var2
         gain = keep.tile([P, CHUNKS], F32)
         scaled = keep.tile([P, CHUNKS, L], F32)
         shift = keep.tile([P, CHUNKS, L], F32)
-        shift_x = keep.tile([P, CHUNKS, ROWS], F32)
 
         def transpose_params():
-            for m in range(CHUNKS):
-                nc.tensor.transpose(params_T[:, m, :], params[:, m * P : (m + 1) * P], ident_bf16[:])
+            nc.tensor.transpose(params_T[:], params[:], ident_bf16[:])
 
         def copy_params():
-            nc.scalar.copy(out=pvals[:], in_=params_T[:, :, 0:6].rearrange("p m v -> p v m"))
+            nc.scalar.copy(out=pvals[:].rearrange("p v m -> p (v m)"), in_=params_T[:, 0 : 6 * CHUNKS])
 
         def take_rstd():
             nc.scalar.activation(out=rstd[:], in_=var_c, func=ACT.Abs_reciprocal_sqrt, bias=BN_EPS)
@@ -199,76 +200,89 @@ def tile_residualblock5_pb_s_kernel(tc, h, x, k2, b2, gamma2, beta2, mean2, var2
         def take_shift():
             nc.vector.tensor_add(out=shift[:], in0=scaled[:], in1=beta_c.unsqueeze(2).to_broadcast([P, CHUNKS, L]))
 
-        def transpose_x():
-            for m in range(CHUNKS):
-                nc.tensor.transpose(x_T[:, m, :], x_rows[:, m * P : (m + 1) * P], ident_bf16[:])
+        u = [keep.tile([P, ROWS], F32, name="u%d" % c) for c in range(CHUNKS)]
+        z_ps = {}
 
-        def add_shift(m):
+        def place_x(g):
+            first, width = GROUPS[g]
+            z_ps[g] = psum.tile([ROWS, width], F32, name="z_ps%d" % g, tag=("z_ps0", "params_T", "h_T")[g])
+            nc.tensor.matmul(
+                out=z_ps[g][:], lhsT=ident_bf16[:], rhs=x_rows[:, first : first + width], start=True, stop=False
+            )
+
+        def normalise_on_scalar(c):
             for l in range(L):
+                half = slice(l * B, (l + 1) * B)
                 nc.scalar.activation(
-                    out=shift_x[:, m, l * B : (l + 1) * B],
-                    in_=x_T[:, m, :].rearrange("p (b l) -> p l b", l=L)[:, l, :],
+                    out=u[c][:, half],
+                    in_=y_ps[c][:, half],
                     func=ACT.Identity,
-                    bias=shift[:, m, l : l + 1],
+                    bias=shift[:, c, l : l + 1],
+                    scale=gain[:, c : c + 1],
                 )
 
-        z = [keep.tile([P, width], F32, name="z%d" % g) for g, (first, width) in enumerate(GROUPS)]
-        res_T = [keep.tile([P, width], F32, name="res_T%d" % g) for g, (first, width) in enumerate(GROUPS)]
+        def normalise_on_vector(c):
+            nc.vector.scalar_tensor_tensor(
+                out=u[c][:].rearrange("p (l b) -> p l b", l=L),
+                in0=y_ps[c][:].rearrange("p (l b) -> p l b", l=L),
+                scalar=gain[:, c : c + 1],
+                in1=shift[:, c, :].unsqueeze(2).to_broadcast([P, L, B]),
+                op0=ALU.mult,
+                op1=ALU.add,
+            )
 
-        def take_z(g):
+        def sum_z(g):
             first, width = GROUPS[g]
             for k in range(width // P):
-                c = first // P + k
-                nc.vector.scalar_tensor_tensor(
-                    out=z[g][:, k * P : (k + 1) * P],
-                    in0=y_ps[c][:],
-                    scalar=gain[:, c : c + 1],
-                    in1=shift_x[:, c, :],
-                    op0=ALU.mult,
-                    op1=ALU.add,
+                nc.tensor.matmul(
+                    out=z_ps[g][:, k * P : (k + 1) * P],
+                    lhsT=u[first // P + k][:],
+                    rhs=ident_f32[:],
+                    is_transpose=True,
+                    start=False,
+                    stop=(k == width // P - 1),
                 )
 
         def finish(g):
             first, width = GROUPS[g]
-            nc.vector.scalar_tensor_tensor(
-                out=res_T[g][:], in0=z[g][:], scalar=LEAKY_ALPHA, in1=z[g][:], op0=ALU.mult, op1=ALU.max
-            )
-            back = psum.tile([ROWS, width], F32, name="back%d" % g, tag=("h_T", "params_T", "x_T")[g])
-            for k in range(width // P):
-                cols = slice(k * P, (k + 1) * P)
-                nc.tensor.transpose(back[:, cols], res_T[g][:, cols], ident_f32[:])
+            small = keep.tile([ROWS, width], F32, name="small%d" % g)
+            nc.scalar.activation(out=small[:], in_=z_ps[g][:], func=ACT.Copy, scale=LEAKY_ALPHA)
             res = keep.tile([ROWS, width], F32, name="res%d" % g)
-            nc.scalar.copy(out=res[:], in_=back[:])
+            nc.vector.tensor_max(out=res[:], in0=z_ps[g][:], in1=small[:])
             for l in range(L):
                 nc.sync.dma_start(out=out[:, l, first : first + width], in_=res[l * B : (l + 1) * B, :])
 
-        after_regroup = {
-            0: (transpose_h, transpose_params, copy_params),
-            1: (take_rstd, copy_h),
-            6: (lambda: add_shift(0), lambda: add_shift(1)),
-            7: (lambda: add_shift(2), lambda: add_shift(3)),
-        }
-        after_quantise = {
-            0: (quantise_h, take_gain),
-            1: (scale_shift,),
-            2: (take_shift,),
-            4: (transpose_x,),
-            5: (move_through_tensor,),
-        }
-
-        for j in range(len(pieces) + 1):
-            if j < len(pieces):
-                regroup_piece(j)
-                for step in after_regroup.get(j, ()):
-                    step()
-            if j > 0:
-                quantise_piece(j - 1)
-                for step in after_quantise.get(j - 1, ()):
-                    step()
-                multiply_piece(j - 1)
-        take_z(0)
-        take_z(1)
+        transpose_h()
+        copy_h()
+        quantise_h()
+        transpose_params()
+        regroup_piece(0)
+        copy_params()
+        take_rstd()
+        take_gain()
+        quantise_piece(0)
+        scale_shift()
+        multiply_piece(0)
+        regroup_piece(1)
+        take_shift()
+        for j in range(1, len(pieces)):
+            if j + 1 < len(pieces):
+                regroup_piece(j + 1)
+            if j == 5:
+                move_through_tensor()
+            quantise_piece(j)
+            multiply_piece(j)
+            if j == 8:
+                for g in range(len(GROUPS)):
+                    place_x(g)
+            if j == 10:
+                normalise_on_scalar(0)
+                normalise_on_scalar(1)
+        sum_z(0)
+        normalise_on_vector(2)
+        sum_z(1)
+        normalise_on_vector(3)
+        sum_z(2)
         finish(0)
-        take_z(2)
         finish(1)
         finish(2)

@@ -65,11 +65,11 @@ def tile_residualblock5_pb_s_kernel(tc, h, x, k2, b2, gamma2, beta2, mean2, var2
         nc.sync.dma_start(out=h_rows[:], in_=h.rearrange("b l c -> (b l) c"))
         load_kernel()
         for v, vec in enumerate((gamma2, beta2, mean2, var2)):
-            nc.sync.dma_start(out=params[v * CHUNKS : (v + 1) * CHUNKS, :], in_=vec.rearrange("(m p) -> m p", p=P))
-        nc.sync.dma_start(out=params[4 * CHUNKS : 6 * CHUNKS, :], in_=b2.rearrange("l (m p) -> (l m) p", p=P))
-        for m in range(1, 4):
             load_kernel()
-        for m in range(4, len(kernels)):
+            nc.sync.dma_start(out=params[v * CHUNKS : (v + 1) * CHUNKS, :], in_=vec.rearrange("(m p) -> m p", p=P))
+        load_kernel()
+        nc.sync.dma_start(out=params[4 * CHUNKS : 6 * CHUNKS, :], in_=b2.rearrange("l (m p) -> (l m) p", p=P))
+        while len(w_raw) < len(kernels):
             load_kernel()
         for l in range(L):
             nc.sync.dma_start(out=x_rows[l * B : (l + 1) * B, :], in_=x[:, l, :])
@@ -255,22 +255,27 @@ def tile_residualblock5_pb_s_kernel(tc, h, x, k2, b2, gamma2, beta2, mean2, var2
         transpose_h()
         copy_h()
         quantise_h()
-        transpose_params()
         regroup_piece(0)
-        copy_params()
-        take_rstd()
-        take_gain()
-        quantise_piece(0)
-        scale_shift()
-        multiply_piece(0)
         regroup_piece(1)
-        take_shift()
+        quantise_piece(0)
+        multiply_piece(0)
         for j in range(1, len(pieces)):
             if j + 1 < len(pieces):
                 regroup_piece(j + 1)
+            if j == 4:
+                transpose_params()
+                copy_params()
             if j == 5:
+                take_rstd()
+            if j == 6:
                 move_through_tensor()
             quantise_piece(j)
+            if j == 6:
+                take_gain()
+            if j == 7:
+                scale_shift()
+            if j == 8:
+                take_shift()
             multiply_piece(j)
             if j == 8:
                 for g in range(len(GROUPS)):

@@ -62,8 +62,8 @@ def tile_residualblock5_pb_s_kernel(tc, h, x, k2, b2, gamma2, beta2, mean2, var2
             nc.sync.dma_start(out=raw[:], in_=k2[i, l].rearrange("(p t) f -> p t f", t=PACK))
             w_raw.append(raw)
 
-        nc.sync.dma_start(out=h_rows[:], in_=h.rearrange("b l c -> (b l) c"))
         load_kernel()
+        nc.sync.dma_start(out=h_rows[:], in_=h.rearrange("b l c -> (b l) c"))
         for v, vec in enumerate((gamma2, beta2, mean2, var2)):
             load_kernel()
             nc.sync.dma_start(out=params[v * CHUNKS : (v + 1) * CHUNKS, :], in_=vec.rearrange("(m p) -> m p", p=P))
@@ -253,11 +253,11 @@ def tile_residualblock5_pb_s_kernel(tc, h, x, k2, b2, gamma2, beta2, mean2, var2
                 nc.sync.dma_start(out=out[:, l, first : first + width], in_=res[l * B : (l + 1) * B, :])
 
         transpose_h()
-        copy_h()
-        quantise_h()
         regroup_piece(0)
-        regroup_piece(1)
+        copy_h()
         quantise_piece(0)
+        regroup_piece(1)
+        quantise_h()
         multiply_piece(0)
         for j in range(1, len(pieces)):
             if j + 1 < len(pieces):

@@ -15,8 +15,6 @@ P = 128
 PACK = 4
 B, L, C, TAPS = 64, 2, 512, 5
 ROWS = B * L
-THROUGH_TENSOR = 8
-MOVED = 128
 STEPS = (0, 0, 1, -1, 2)
 CHUNKS = C // P
 BN_EPS = 1e-3
@@ -110,32 +108,14 @@ def tile_residualblock5_pb_s_kernel(tc, h, x, k2, b2, gamma2, beta2, mean2, var2
         w_codes = [keep.tile([P, C], U32, name="w_codes%d" % m, align_bytes=64) for m in range(len(kernels))]
         w_scales = [keep.tile([P, C], U8, name="w_scales%d" % m, align_bytes=64) for m in range(len(kernels))]
         grouped_of = {}
-        moved_of = {}
 
         def regroup_piece(j):
             m, first, width = pieces[j]
             vector_cols = VECTOR_COLS_FIRST if j == 0 else VECTOR_COLS[width]
             grouped = stage.tile([P, C, PACK], BF16, align_bytes=64)
             regroup(nc.vector.tensor_copy, grouped, w_raw[m], slice(first, first + vector_cols))
-            scalar_first = first + vector_cols
-            if m == THROUGH_TENSOR:
-                nc.scalar.copy(out=grouped[:, scalar_first : scalar_first + MOVED, :], in_=moved_of[m][:])
-                scalar_first += MOVED
-            regroup(nc.scalar.copy, grouped, w_raw[m], slice(scalar_first, first + width))
+            regroup(nc.scalar.copy, grouped, w_raw[m], slice(first + vector_cols, first + width))
             grouped_of[j] = grouped
-
-        def move_through_tensor():
-            first = VECTOR_COLS[C]
-            moved = psum.tile([P, MOVED, PACK], BF16)
-            for f in range(0, MOVED, P):
-                nc.tensor.matmul(
-                    out=moved[:, f : f + P, :].rearrange("p f t -> p (f t)"),
-                    lhsT=ident_bf16[:],
-                    rhs=w_raw[THROUGH_TENSOR][:, :, first + f : first + f + P].rearrange("p t f -> p f t"),
-                    start=True,
-                    stop=True,
-                )
-            moved_of[THROUGH_TENSOR] = moved
 
         def quantise_piece(j):
             m, first, width = pieces[j]
@@ -243,14 +223,17 @@ def tile_residualblock5_pb_s_kernel(tc, h, x, k2, b2, gamma2, beta2, mean2, var2
                     stop=(k == width // P - 1),
                 )
 
+        small = [keep.tile([ROWS, width], F32, name="small%d" % g) for g, (first, width) in enumerate(GROUPS)]
+
+        def shrink(g):
+            nc.scalar.activation(out=small[g][:], in_=z_ps[g][:], func=ACT.Copy, scale=LEAKY_ALPHA)
+
         def finish(g):
             first, width = GROUPS[g]
-            small = keep.tile([ROWS, width], F32, name="small%d" % g)
-            nc.scalar.activation(out=small[:], in_=z_ps[g][:], func=ACT.Copy, scale=LEAKY_ALPHA)
             res = keep.tile([ROWS, width], F32, name="res%d" % g)
-            nc.vector.tensor_max(out=res[:], in0=z_ps[g][:], in1=small[:])
-            for l in range(L):
-                nc.sync.dma_start(out=out[:, l, first : first + width], in_=res[l * B : (l + 1) * B, :])
+            nc.vector.tensor_max(out=res[:], in0=z_ps[g][:], in1=small[g][:])
+            for l, queue in enumerate((nc.sync, nc.scalar)):
+                queue.dma_start(out=out[:, l, first : first + width], in_=res[l * B : (l + 1) * B, :])
 
         transpose_h()
         regroup_piece(0)
@@ -267,8 +250,6 @@ def tile_residualblock5_pb_s_kernel(tc, h, x, k2, b2, gamma2, beta2, mean2, var2
                 copy_params()
             if j == 5:
                 take_rstd()
-            if j == 6:
-                move_through_tensor()
             quantise_piece(j)
             if j == 6:
                 take_gain()
@@ -277,17 +258,20 @@ def tile_residualblock5_pb_s_kernel(tc, h, x, k2, b2, gamma2, beta2, mean2, var2
             if j == 8:
                 take_shift()
             multiply_piece(j)
-            if j == 8:
-                for g in range(len(GROUPS)):
-                    place_x(g)
+            if j == 9:
+                place_x(0)
             if j == 10:
                 normalise_on_scalar(0)
                 normalise_on_scalar(1)
+                place_x(1)
+                place_x(2)
         sum_z(0)
         normalise_on_vector(2)
-        sum_z(1)
         normalise_on_vector(3)
+        sum_z(1)
         sum_z(2)
+        for g in range(len(GROUPS)):
+            shrink(g)
         finish(0)
         finish(1)
         finish(2)

@@ -19,6 +19,7 @@ STEPS = (0, 0, 1, -1, 2)
 CHUNKS = C // P
 BN_EPS = 1e-3
 LEAKY_ALPHA = 0.3
+WARM_COLS = 256
 RUN = 4
 VECTOR_COLS = {512: 248, 256: 96, 128: 48}
 VECTOR_COLS_FIRST = 336
@@ -144,6 +145,21 @@ def tile_residualblock5_pb_s_kernel(tc, h, x, k2, b2, gamma2, beta2, mean2, var2
                     stop=(m == last),
                 )
 
+        scratch = psum.tile([P, WARM_COLS], F32)
+
+        def keep_warm(m):
+            for c in range(2):
+                chunk = slice(c * P, (c + 1) * P)
+                nc.tensor.matmul_mx(
+                    out=scratch[:],
+                    lhsT=w_codes[m][:, chunk].bitcast(FP8X4),
+                    lhsT_scale=w_scales[m][:, chunk],
+                    rhs=h_codes[:, 0:WARM_COLS].bitcast(FP8X4),
+                    rhs_scale=h_scales[:, 0:WARM_COLS],
+                    start=True,
+                    stop=True,
+                )
+
         params_T = psum.tile([P, P], BF16)
         pvals = keep.tile([P, 6, CHUNKS], F32)
         gamma_c, beta_c, mean_c, var_c = pvals[:, 0, :], pvals[:, 1, :], pvals[:, 2, :], pvals[:, 3, :]
@@ -242,22 +258,26 @@ def tile_residualblock5_pb_s_kernel(tc, h, x, k2, b2, gamma2, beta2, mean2, var2
         regroup_piece(1)
         quantise_h()
         multiply_piece(0)
+        keep_warm(0)
         for j in range(1, len(pieces)):
             if j + 1 < len(pieces):
                 regroup_piece(j + 1)
             if j == 4:
                 transpose_params()
-                copy_params()
             if j == 5:
+                copy_params()
+            if j == 6:
                 take_rstd()
             quantise_piece(j)
-            if j == 6:
-                take_gain()
             if j == 7:
-                scale_shift()
+                take_gain()
             if j == 8:
+                scale_shift()
+            if j == 9:
                 take_shift()
             multiply_piece(j)
+            if j < last - 1:
+                keep_warm(j)
             if j == 9:
                 place_x(0)
             if j == 10:

@@ -58,7 +58,9 @@ def tile_residualblock5_pb_s_kernel(tc, h, x, k2, b2, gamma2, beta2, mean2, var2
         def load_kernel():
             i, l = kernels[len(w_raw)]
             raw = keep.tile([P, PACK, C], BF16, name="w_raw%d" % len(w_raw))
-            nc.sync.dma_start(out=raw[:], in_=k2[i, l].rearrange("(p t) f -> p t f", t=PACK))
+            nc.sync.dma_start(
+                out=raw[:].rearrange("p t f -> p (t f)"), in_=k2[i, l].rearrange("(p t) f -> p (t f)", t=PACK)
+            )
             w_raw.append(raw)
 
         load_kernel()

@@ -50,14 +50,14 @@ def tile_residualblock5_pb_s_kernel(tc, h, x, k2, b2, gamma2, beta2, mean2, var2
 
         params = keep.tile([P, P], BF16)
         nc.vector.memset(params[:], 0.0)
-        h_rows = keep.tile([ROWS, C], BF16)
-        x_rows = keep.tile([ROWS, C], BF16)
+        h_rows = keep.tile([ROWS, C], BF16, align_bytes=512)
+        x_rows = keep.tile([ROWS, C], BF16, align_bytes=512)
         kernels = [(i, l) for i in range(TAPS) for l in range(L)]
         w_raw = []
 
         def load_kernel():
             i, l = kernels[len(w_raw)]
-            raw = keep.tile([P, PACK, C], BF16, name="w_raw%d" % len(w_raw))
+            raw = keep.tile([P, PACK, C], BF16, name="w_raw%d" % len(w_raw), align_bytes=512)
             nc.sync.dma_start(
                 out=raw[:].rearrange("p t f -> p (t f)"), in_=k2[i, l].rearrange("(p t) f -> p (t f)", t=PACK)
             )
@@ -147,7 +147,7 @@ def tile_residualblock5_pb_s_kernel(tc, h, x, k2, b2, gamma2, beta2, mean2, var2
                     stop=(m == last),
                 )
 
-        scratch = psum.tile([P, WARM_COLS], F32)
+        scratch = psum.tile([P, WARM_COLS], F32, tag="z_ps0")
 
         def keep_warm(m):
             for c in range(2):
@@ -201,11 +201,10 @@ def tile_residualblock5_pb_s_kernel(tc, h, x, k2, b2, gamma2, beta2, mean2, var2
         u = [keep.tile([P, ROWS], F32, name="u%d" % c) for c in range(CHUNKS)]
         z_ps = {}
 
-        def place_x(g):
-            first, width = GROUPS[g]
-            z_ps[g] = psum.tile([ROWS, width], F32, name="z_ps%d" % g, tag=("z_ps0", "params_T", "h_T")[g])
+        def place_x(c):
+            z_ps[c] = psum.tile([ROWS, P], F32, name="z_ps%d" % c, tag=("z_ps0", "z_ps1", "params_T", "h_T")[c])
             nc.tensor.matmul(
-                out=z_ps[g][:], lhsT=ident_bf16[:], rhs=x_rows[:, first : first + width], start=True, stop=False
+                out=z_ps[c][:], lhsT=ident_bf16[:], rhs=x_rows[:, c * P : (c + 1) * P], start=True, stop=False
             )
 
         def normalise_on_scalar(c):
@@ -229,29 +228,26 @@ def tile_residualblock5_pb_s_kernel(tc, h, x, k2, b2, gamma2, beta2, mean2, var2
                 op1=ALU.add,
             )
 
-        def sum_z(g):
+        def sum_z(c):
+            nc.tensor.matmul(
+                out=z_ps[c][:], lhsT=u[c][:], rhs=ident_f32[:], is_transpose=True, start=False, stop=True
+            )
+
+        small = [keep.tile([ROWS, P], F32, name="small%d" % c) for c in range(CHUNKS)]
+        res = [keep.tile([ROWS, width], F32, name="res%d" % g) for g, (first, width) in enumerate(GROUPS)]
+
+        def shrink(c):
+            nc.scalar.activation(out=small[c][:], in_=z_ps[c][:], func=ACT.Copy, scale=LEAKY_ALPHA)
+
+        def take_max(c):
+            g = max(k for k, (first, width) in enumerate(GROUPS) if first <= c * P)
+            at = c * P - GROUPS[g][0]
+            nc.vector.tensor_max(out=res[g][:, at : at + P], in0=z_ps[c][:], in1=small[c][:])
+
+        def store(g):
             first, width = GROUPS[g]
-            for k in range(width // P):
-                nc.tensor.matmul(
-                    out=z_ps[g][:, k * P : (k + 1) * P],
-                    lhsT=u[first // P + k][:],
-                    rhs=ident_f32[:],
-                    is_transpose=True,
-                    start=False,
-                    stop=(k == width // P - 1),
-                )
-
-        small = [keep.tile([ROWS, width], F32, name="small%d" % g) for g, (first, width) in enumerate(GROUPS)]
-
-        def shrink(g):
-            nc.scalar.activation(out=small[g][:], in_=z_ps[g][:], func=ACT.Copy, scale=LEAKY_ALPHA)
-
-        def finish(g):
-            first, width = GROUPS[g]
-            res = keep.tile([ROWS, width], F32, name="res%d" % g)
-            nc.vector.tensor_max(out=res[:], in0=z_ps[g][:], in1=small[g][:])
             for l, queue in enumerate((nc.sync, nc.scalar)):
-                queue.dma_start(out=out[:, l, first : first + width], in_=res[l * B : (l + 1) * B, :])
+                queue.dma_start(out=out[:, l, first : first + width], in_=res[g][l * B : (l + 1) * B, :])
 
         transpose_h()
         regroup_piece(0)
@@ -261,39 +257,49 @@ def tile_residualblock5_pb_s_kernel(tc, h, x, k2, b2, gamma2, beta2, mean2, var2
         quantise_h()
         multiply_piece(0)
         keep_warm(0)
-        for j in range(1, len(pieces)):
-            if j + 1 < len(pieces):
-                regroup_piece(j + 1)
+        for j in range(1, last):
+            regroup_piece(j + 1)
             if j == 4:
-                transpose_params()
-            if j == 5:
                 copy_params()
-            if j == 6:
+            if j == 5:
                 take_rstd()
             quantise_piece(j)
-            if j == 7:
+            if j == 5:
                 take_gain()
-            if j == 8:
+            if j == 6:
                 scale_shift()
-            if j == 9:
+            if j == 7:
                 take_shift()
+            if j == 8:
+                for c in range(CHUNKS):
+                    place_x(c)
             multiply_piece(j)
-            if j < last - 1:
+            if j <= 6:
                 keep_warm(j)
-            if j == 9:
-                place_x(0)
-            if j == 10:
-                normalise_on_scalar(0)
-                normalise_on_scalar(1)
-                place_x(1)
-                place_x(2)
+            if j == 3:
+                transpose_params()
+        regroup_piece(last + 1)
+        quantise_piece(last)
+        multiply_piece(last)
+        regroup_piece(last + 2)
+        quantise_piece(last + 1)
+        multiply_piece(last + 1)
+        normalise_on_scalar(0)
+        normalise_on_scalar(1)
+        quantise_piece(last + 2)
+        multiply_piece(last + 2)
         sum_z(0)
+        sum_z(1)
         normalise_on_vector(2)
         normalise_on_vector(3)
-        sum_z(1)
         sum_z(2)
-        for g in range(len(GROUPS)):
-            shrink(g)
-        finish(0)
-        finish(1)
-        finish(2)
+        sum_z(3)
+        for c in range(CHUNKS):
+            shrink(c)
+        take_max(0)
+        take_max(1)
+        store(0)
+        take_max(2)
+        store(1)
+        take_max(3)
+        store(2)

@@ -72,8 +72,7 @@ def tile_residualblock5_pb_s_kernel(tc, h, x, k2, b2, gamma2, beta2, mean2, var2
         nc.sync.dma_start(out=params[4 * CHUNKS : 6 * CHUNKS, :], in_=b2.rearrange("l (m p) -> (l m) p", p=P))
         while len(w_raw) < len(kernels):
             load_kernel()
-        for l in range(L):
-            nc.sync.dma_start(out=x_rows[l * B : (l + 1) * B, :], in_=x[:, l, :])
+        nc.sync.dma_start(out=x_rows[:], in_=x.rearrange("b l c -> (b l) c"))
 
         ident_f32 = keep.tile([P, P], F32)
         make_identity(nc, ident_f32[:])
@@ -207,23 +206,12 @@ def tile_residualblock5_pb_s_kernel(tc, h, x, k2, b2, gamma2, beta2, mean2, var2
                 out=z_ps[c][:], lhsT=ident_bf16[:], rhs=x_rows[:, c * P : (c + 1) * P], start=True, stop=False
             )
 
-        def normalise_on_scalar(c):
-            for l in range(L):
-                half = slice(l * B, (l + 1) * B)
-                nc.scalar.activation(
-                    out=u[c][:, half],
-                    in_=y_ps[c][:, half],
-                    func=ACT.Identity,
-                    bias=shift[:, c, l : l + 1],
-                    scale=gain[:, c : c + 1],
-                )
-
-        def normalise_on_vector(c):
+        def normalise(c):
             nc.vector.scalar_tensor_tensor(
-                out=u[c][:].rearrange("p (l b) -> p l b", l=L),
-                in0=y_ps[c][:].rearrange("p (l b) -> p l b", l=L),
+                out=u[c][:].rearrange("p (b l) -> p b l", l=L),
+                in0=y_ps[c][:].rearrange("p (l b) -> p b l", l=L),
                 scalar=gain[:, c : c + 1],
-                in1=shift[:, c, :].unsqueeze(2).to_broadcast([P, L, B]),
+                in1=shift[:, c, :].unsqueeze(1).to_broadcast([P, B, L]),
                 op0=ALU.mult,
                 op1=ALU.add,
             )
@@ -234,20 +222,19 @@ def tile_residualblock5_pb_s_kernel(tc, h, x, k2, b2, gamma2, beta2, mean2, var2
             )
 
         small = [keep.tile([ROWS, P], F32, name="small%d" % c) for c in range(CHUNKS)]
-        res = [keep.tile([ROWS, width], F32, name="res%d" % g) for g, (first, width) in enumerate(GROUPS)]
+        res = [keep.tile([ROWS, C // 2], F32, name="res%d" % k) for k in range(2)]
 
         def shrink(c):
             nc.scalar.activation(out=small[c][:], in_=z_ps[c][:], func=ACT.Copy, scale=LEAKY_ALPHA)
 
         def take_max(c):
-            g = max(k for k, (first, width) in enumerate(GROUPS) if first <= c * P)
-            at = c * P - GROUPS[g][0]
-            nc.vector.tensor_max(out=res[g][:, at : at + P], in0=z_ps[c][:], in1=small[c][:])
+            cols = slice(c % 2 * P, (c % 2 + 1) * P)
+            nc.vector.tensor_max(out=res[c // 2][:, cols], in0=z_ps[c][:], in1=small[c][:])
 
-        def store(g):
-            first, width = GROUPS[g]
-            for l, queue in enumerate((nc.sync, nc.scalar)):
-                queue.dma_start(out=out[:, l, first : first + width], in_=res[g][l * B : (l + 1) * B, :])
+        def store(k):
+            nc.sync.dma_start(
+                out=out.rearrange("b l f -> (b l) f")[:, k * C // 2 : (k + 1) * C // 2], in_=res[k][:]
+            )
 
         transpose_h()
         regroup_piece(0)
@@ -284,22 +271,16 @@ def tile_residualblock5_pb_s_kernel(tc, h, x, k2, b2, gamma2, beta2, mean2, var2
         regroup_piece(last + 2)
         quantise_piece(last + 1)
         multiply_piece(last + 1)
-        normalise_on_scalar(0)
-        normalise_on_scalar(1)
         quantise_piece(last + 2)
         multiply_piece(last + 2)
-        sum_z(0)
-        sum_z(1)
-        normalise_on_vector(2)
-        normalise_on_vector(3)
-        sum_z(2)
-        sum_z(3)
+        for c in range(CHUNKS):
+            normalise(c)
+            sum_z(c)
         for c in range(CHUNKS):
             shrink(c)
         take_max(0)
         take_max(1)
         store(0)
         take_max(2)
-        store(1)
         take_max(3)
-        store(2)
+        store(1)

from contextlib import ExitStack

import concourse.mybir as mybir
from concourse.masks import make_identity

F32 = mybir.dt.float32
BF16 = mybir.dt.bfloat16
U32 = mybir.dt.uint32
U8 = mybir.dt.uint8
FP8X4 = mybir.dt.float8_e4m3fn_x4
ALU = mybir.AluOpType
ACT = mybir.ActivationFunctionType

P = 128
PACK = 4
B, L, C, TAPS = 64, 2, 512, 5
ROWS = B * L
STEPS = (0, 0, 1, -1, 2)
CHUNKS = C // P
BN_EPS = 1e-3
LEAKY_ALPHA = 0.3
WARM_COLS = 256
RUN = 4
VECTOR_COLS = {512: 248, 256: 96, 128: 48}
VECTOR_COLS_FIRST = 336
GROUPS = ((0, C // 2), (C // 2, C // 4), (3 * C // 4, C // 4))

FLOPS = 2 * B * L * TAPS * C * C


def regroup(copy, grouped, raw, cols):
    copy(
        out=grouped[:, cols, :].rearrange("p (c i) t -> p c t i", i=RUN),
        in_=raw[:, :, cols].rearrange("p t (c i) -> p c t i", i=RUN),
    )


def tile_residualblock5_pb_s_kernel(tc, h, x, k2, b2, gamma2, beta2, mean2, var2, out):
    nc = tc.nc
    with ExitStack() as ctx:
        keep = ctx.enter_context(tc.tile_pool(name="keep", bufs=1))
        stage = ctx.enter_context(tc.tile_pool(name="stage", bufs=4))
        psum = ctx.enter_context(tc.psum_pool(name="psum", bufs=1))
        ctx.enter_context(tc.manual_schedule())

        one = keep.tile([P, 1], F32)
        nc.vector.memset(one[:], 1.0)
        warm = keep.tile([P, 1], F32)
        nc.scalar.activation(out=warm[:], in_=one[:], func=ACT.Abs_reciprocal_sqrt)

        params = keep.tile([P, P], BF16)
        nc.vector.memset(params[:], 0.0)
        h_rows = keep.tile([ROWS, C], BF16, align_bytes=512)
        x_rows = keep.tile([ROWS, C], BF16, align_bytes=512)
        kernels = [(i, l) for i in range(TAPS) for l in range(L)]
        w_raw = []

        def load_kernel():
            i, l = kernels[len(w_raw)]
            raw = keep.tile([P, PACK, C], BF16, name="w_raw%d" % len(w_raw), align_bytes=512)
            nc.sync.dma_start(
                out=raw[:].rearrange("p t f -> p (t f)"), in_=k2[i, l].rearrange("(p t) f -> p (t f)", t=PACK)
            )
            w_raw.append(raw)

        load_kernel()
        nc.sync.dma_start(out=h_rows[:], in_=h.rearrange("b l c -> (b l) c"))
        for v, vec in enumerate((gamma2, beta2, mean2, var2)):
            load_kernel()
            nc.sync.dma_start(out=params[v * CHUNKS : (v + 1) * CHUNKS, :], in_=vec.rearrange("(m p) -> m p", p=P))
        load_kernel()
        nc.sync.dma_start(out=params[4 * CHUNKS : 6 * CHUNKS, :], in_=b2.rearrange("l (m p) -> (l m) p", p=P))
        while len(w_raw) < len(kernels):
            load_kernel()
        nc.sync.dma_start(out=x_rows[:], in_=x.rearrange("b l c -> (b l) c"))

        ident_f32 = keep.tile([P, P], F32)
        make_identity(nc, ident_f32[:])
        ident_bf16 = keep.tile([P, P], BF16)
        make_identity(nc, ident_bf16[:])

        h_words = h_rows[:].bitcast(F32).rearrange("r (p u) -> r u p", u=2)
        h_codes = keep.tile([P, (2 * L + 1) * B], U32, align_bytes=64)
        h_scales = keep.tile([P, (2 * L + 1) * B], U8, align_bytes=64)
        nc.vector.memset(h_codes[:].rearrange("p (g b) -> p g b", b=B)[:, 0::2, :], 0)
        nc.vector.memset(h_scales[:].bitcast(U32).rearrange("p (g b) -> p g b", b=B // PACK)[:, 0::2, :], 0)
        h_T = psum.tile([P, 2, ROWS], F32)
        h_grouped = keep.tile([P, L, B * PACK], BF16, align_bytes=64)

        def transpose_h():
            for u in range(2):
                nc.tensor.transpose(h_T[:, u, :], h_words[:, u, :], ident_f32[:])

        def copy_h():
            nc.scalar.copy(
                out=h_grouped[:].rearrange("p s w -> p (s w)").bitcast(F32).rearrange("p (s b u) -> p s b u", s=L, u=2),
                in_=h_T[:].rearrange("p u (b s) -> p s b u", s=L),
            )

        def quantise_h():
            for source in range(L):
                live = slice((2 * source + 1) * B, (2 * source + 2) * B)
                nc.vector.quantize_mx(
                    out=h_codes[:, live].bitcast(FP8X4), scales=h_scales[:, live], in_=h_grouped[:, source, :]
                )

        last = len(kernels) - 1
        pieces = [(m, 0, C) for m in range(last)] + [(last, first, width) for first, width in GROUPS]
        y_ps = [psum.tile([P, ROWS], F32, name="y_ps%d" % c) for c in range(CHUNKS)]
        w_codes = [keep.tile([P, C], U32, name="w_codes%d" % m, align_bytes=64) for m in range(len(kernels))]
        w_scales = [keep.tile([P, C], U8, name="w_scales%d" % m, align_bytes=64) for m in range(len(kernels))]
        grouped_of = {}

        def regroup_piece(j):
            m, first, width = pieces[j]
            vector_cols = VECTOR_COLS_FIRST if j == 0 else VECTOR_COLS[width]
            grouped = stage.tile([P, C, PACK], BF16, align_bytes=64)
            regroup(nc.vector.tensor_copy, grouped, w_raw[m], slice(first, first + vector_cols))
            regroup(nc.scalar.copy, grouped, w_raw[m], slice(first + vector_cols, first + width))
            grouped_of[j] = grouped

        def quantise_piece(j):
            m, first, width = pieces[j]
            cols = slice(first, first + width)
            nc.vector.quantize_mx(
                out=w_codes[m][:, cols].bitcast(FP8X4),
                scales=w_scales[m][:, cols],
                in_=grouped_of[j][:, cols, :].rearrange("p f t -> p (f t)"),
            )

        def multiply_piece(j):
            m, first, width = pieces[j]
            i, l = kernels[m]
            source = (l - STEPS[i]) % L
            operand_first = (2 * source + 1 - l) * B
            operand = slice(operand_first, operand_first + ROWS)
            for c in range(first // P, (first + width) // P):
                chunk = slice(c * P, (c + 1) * P)
                nc.tensor.matmul_mx(
                    out=y_ps[c][:],
                    lhsT=w_codes[m][:, chunk].bitcast(FP8X4),
                    lhsT_scale=w_scales[m][:, chunk],
                    rhs=h_codes[:, operand].bitcast(FP8X4),
                    rhs_scale=h_scales[:, operand],
                    start=(m == 0),
                    stop=(m == last),
                )

        scratch = psum.tile([P, WARM_COLS], F32, tag="z_ps0")

        def keep_warm(m):
            for c in range(2):
                chunk = slice(c * P, (c + 1) * P)
                nc.tensor.matmul_mx(
                    out=scratch[:],
                    lhsT=w_codes[m][:, chunk].bitcast(FP8X4),
                    lhsT_scale=w_scales[m][:, chunk],
                    rhs=h_codes[:, 0:WARM_COLS].bitcast(FP8X4),
                    rhs_scale=h_scales[:, 0:WARM_COLS],
                    start=True,
                    stop=True,
                )

        params_T = psum.tile([P, P], BF16)
        pvals = keep.tile([P, 6, CHUNKS], F32)
        gamma_c, beta_c, mean_c, var_c = pvals[:, 0, :], pvals[:, 1, :], pvals[:, 2, :], pvals[:, 3, :]
        b2_c = pvals[:, 4:6, :].rearrange("p l m -> p m l")
        rstd = keep.tile([P, CHUNKS], F32)
        centred = keep.tile([P, CHUNKS, L], F32)
        gain = keep.tile([P, CHUNKS], F32)
        scaled = keep.tile([P, CHUNKS, L], F32)
        shift = keep.tile([P, CHUNKS, L], F32)

        def transpose_params():
            nc.tensor.transpose(params_T[:], params[:], ident_bf16[:])

        def copy_params():
            nc.scalar.copy(out=pvals[:].rearrange("p v m -> p (v m)"), in_=params_T[:, 0 : 6 * CHUNKS])

        def take_rstd():
            nc.scalar.activation(out=rstd[:], in_=var_c, func=ACT.Abs_reciprocal_sqrt, bias=BN_EPS)

        def take_gain():
            nc.vector.scalar_tensor_tensor(
                out=centred[:],
                in0=b2_c,
                scalar=2.0,
                in1=mean_c.unsqueeze(2).to_broadcast([P, CHUNKS, L]),
                op0=ALU.mult,
                op1=ALU.subtract,
            )
            nc.vector.tensor_mul(out=gain[:], in0=gamma_c, in1=rstd[:])

        def scale_shift():
            nc.vector.tensor_mul(out=scaled[:], in0=centred[:], in1=gain[:].unsqueeze(2).to_broadcast([P, CHUNKS, L]))

        def take_shift():
            nc.vector.tensor_add(out=shift[:], in0=scaled[:], in1=beta_c.unsqueeze(2).to_broadcast([P, CHUNKS, L]))

        u = [keep.tile([P, ROWS], F32, name="u%d" % c) for c in range(CHUNKS)]
        z_ps = {}

        def place_x(c):
            z_ps[c] = psum.tile([ROWS, P], F32, name="z_ps%d" % c, tag=("z_ps0", "z_ps1", "params_T", "h_T")[c])
            nc.tensor.matmul(
                out=z_ps[c][:], lhsT=ident_bf16[:], rhs=x_rows[:, c * P : (c + 1) * P], start=True, stop=False
            )

        def normalise(c):
            nc.vector.scalar_tensor_tensor(
                out=u[c][:].rearrange("p (b l) -> p b l", l=L),
                in0=y_ps[c][:].rearrange("p (l b) -> p b l", l=L),
                scalar=gain[:, c : c + 1],
                in1=shift[:, c, :].unsqueeze(1).to_broadcast([P, B, L]),
                op0=ALU.mult,
                op1=ALU.add,
            )

        def sum_z(c):
            nc.tensor.matmul(
                out=z_ps[c][:], lhsT=u[c][:], rhs=ident_f32[:], is_transpose=True, start=False, stop=True
            )

        small = [keep.tile([ROWS, P], F32, name="small%d" % c) for c in range(CHUNKS)]
        res = [keep.tile([ROWS, C // 2], F32, name="res%d" % k) for k in range(2)]

        def shrink(c):
            nc.scalar.activation(out=small[c][:], in_=z_ps[c][:], func=ACT.Copy, scale=LEAKY_ALPHA)

        def take_max(c):
            cols = slice(c % 2 * P, (c % 2 + 1) * P)
            nc.vector.tensor_max(out=res[c // 2][:, cols], in0=z_ps[c][:], in1=small[c][:])

        def store(k):
            nc.sync.dma_start(
                out=out.rearrange("b l f -> (b l) f")[:, k * C // 2 : (k + 1) * C // 2], in_=res[k][:]
            )

        transpose_h()
        regroup_piece(0)
        copy_h()
        quantise_piece(0)
        regroup_piece(1)
        quantise_h()
        multiply_piece(0)
        keep_warm(0)
        for j in range(1, last):
            regroup_piece(j + 1)
            if j == 4:
                copy_params()
            if j == 5:
                take_rstd()
            quantise_piece(j)
            if j == 5:
                take_gain()
            if j == 6:
                scale_shift()
            if j == 7:
                take_shift()
            if j == 8:
                for c in range(CHUNKS):
                    place_x(c)
            multiply_piece(j)
            if j <= 6:
                keep_warm(j)
            if j == 3:
                transpose_params()
        regroup_piece(last + 1)
        quantise_piece(last)
        multiply_piece(last)
        regroup_piece(last + 2)
        quantise_piece(last + 1)
        multiply_piece(last + 1)
        quantise_piece(last + 2)
        multiply_piece(last + 2)
        for c in range(CHUNKS):
            normalise(c)
            sum_z(c)
        for c in range(CHUNKS):
            shrink(c)
        take_max(0)
        take_max(1)
        store(0)
        take_max(2)
        take_max(3)
        store(1)
